import numpy as np
import ml_dtypes


def mxq(x, axis, fmt="e4m3"):
    dtype, down = {"e4m3": (ml_dtypes.float8_e4m3fn, 7), "e5m2": (ml_dtypes.float8_e5m2, 14)}[fmt]
    v = np.moveaxis(np.asarray(x, np.float32).astype(ml_dtypes.bfloat16).astype(np.float64), axis, -1)
    blocks = v.reshape(v.shape[:-1] + (-1, 32))
    amax = np.abs(blocks).max(-1, keepdims=True)
    byte = np.maximum(np.where(amax > 0, np.frexp(amax)[1] - 1 + 127, 0) - down, 1)
    scale = np.exp2(byte - 127.0)
    codes = (blocks / scale).astype(np.float32).astype(dtype).astype(np.float64)
    return np.moveaxis((codes * scale).reshape(v.shape), -1, axis)


WIDE = False


def mx_kscale(k):
    if not WIDE:
        return np.ones(k)
    levels = np.array([10, -10, 5, -5, 0])
    a = np.random.permutation(np.resize(levels, k // 512 * 4)).reshape(k // 512, 4)
    idx = np.arange(k)
    return np.exp2(a[idx // 512, idx % 128 // 32])


BF16 = ml_dtypes.bfloat16


def bf(x):
    return np.asarray(x, np.float32).astype(BF16)


def f64(x):
    return np.asarray(x).astype(np.float64)


E2M1 = np.array([0.0, 0.5, 1.0, 1.5, 2.0, 3.0, 4.0, 6.0, -0.0, -0.5, -1.0, -1.5, -2.0, -3.0, -4.0, -6.0])


def pack_weight(w, fmt):
    k, n = w.shape
    w = f64(bf(w)).reshape(k // 32, 32, n)
    amax = np.abs(w).max(1)
    if fmt == "e4m3":
        byte = np.frexp(amax)[1] - 1 + 127 - 7
    else:
        mant, ex = np.frexp(amax / 6.0)
        byte = np.where(mant > 0.5, ex, ex - 1) + 127
    byte = np.clip(np.where(amax > 0, byte, 1), 1, 254)
    scaled = (w * np.exp2(127.0 - byte)[:, None, :]).reshape(k, n).astype(np.float32)
    by_word = np.ascontiguousarray(scaled.reshape(k // 512, 128, 4, n).transpose(0, 1, 3, 2))
    if fmt == "e4m3":
        words = by_word.astype(ml_dtypes.float8_e4m3fn).view(np.uint8)
    else:
        c = by_word.astype(ml_dtypes.float4_e2m1fn).view(np.uint8) & 0xF
        words = c[..., 0::2] | (c[..., 1::2] << 4)
    return np.ascontiguousarray(words), np.ascontiguousarray(byte.astype(np.uint8).reshape(k // 512, 16, n))


def unpack_weight(words, scales, fmt):
    g, p, n, _ = words.shape
    if fmt == "e4m3":
        vals = np.ascontiguousarray(words).view(ml_dtypes.float8_e4m3fn).astype(np.float64)
    else:
        nib = np.empty((g, p, n, 4), np.uint8)
        nib[..., 0::2] = words & 0xF
        nib[..., 1::2] = words >> 4
        vals = E2M1[nib]
    vals = vals * np.repeat(np.exp2(scales.astype(np.float64) - 127.0), 8, axis=1)[..., None]
    return vals.transpose(0, 1, 3, 2).reshape(g * 512, n)


N, C, D, H, W, NHEADS, KSIZE = 1, 16384, 256, 16, 16, 8, 5
PAD = KSIZE // 2
HD = D // NHEADS
WIN = KSIZE * KSIZE
FMT = "e4m3"


def _patches(t):
    tp = np.pad(t, ((0, 0), (0, 0), (PAD, PAD), (PAD, PAD)))
    return np.stack([tp[:, :, i:i + H, j:j + W] for i in range(KSIZE) for j in range(KSIZE)], axis=2)


def setup_inputs():
    s = mx_kscale(C)
    a = np.sqrt(1.5) / HD ** 0.25
    g = np.concatenate([np.full(2 * D, a), np.ones(D)])
    x = bf(np.random.standard_normal((N, C, H, W)) * s[None, :, None, None])
    w = np.random.standard_normal((3 * D, C)) * g[:, None] / np.sqrt(C) / s[None, :]
    words, scales = pack_weight(np.ascontiguousarray(w.T), FMT)
    return {"x": x, "w_qkv_words": words, "w_qkv_scales": scales}


def reference(x, w_qkv_words, w_qkv_scales):
    xq = mxq(f64(x).reshape(N, C, H * W), 1, "e4m3")
    wq = unpack_weight(w_qkv_words, w_qkv_scales, FMT).T
    qkv = (wq @ xq).reshape(N, 3 * D, H, W)
    Q, K, V = np.split(qkv, 3, axis=1)
    Qh = Q.reshape(N, NHEADS, HD, 1, H, W)
    scores = np.sum(_patches(K).reshape(N, NHEADS, HD, WIN, H, W) * Qh, axis=2, keepdims=True)
    e = np.exp(scores - scores.max(axis=3, keepdims=True))
    att = e / e.sum(axis=3, keepdims=True)
    out = np.sum(_patches(V).reshape(N, NHEADS, HD, WIN, H, W) * att, axis=3).reshape(N, D, H, W)
    return out

@@ -1,0 +1,284 @@
+from contextlib import ExitStack
+
+import concourse.mybir as mybir
+
+F32 = mybir.dt.float32
+BF16 = mybir.dt.bfloat16
+I32 = mybir.dt.int32
+U32 = mybir.dt.uint32
+U8 = mybir.dt.uint8
+FP8X4 = mybir.dt.float8_e4m3fn_x4
+ALU = mybir.AluOpType
+ACT = mybir.ActivationFunctionType
+AXIS_X = mybir.AxisListType.X
+
+P = 128
+PACK = 4
+C_IN = 16384
+PASSES = C_IN // (P * PACK)
+PIX = 256
+WIDTH = 16
+D = 256
+HALVES = D // P
+HEADS_T = 4
+HD = 32
+GRP = 32
+NGRP = PIX // GRP
+WIN = 3 * GRP
+CHUNK = 4
+NCHUNK = PASSES // CHUNK
+BANK = 512
+S_PER_BANK = 4
+FAR = -1.0e30
+
+FLOPS = 2 * C_IN * 3 * D * PIX + 2 * 2 * PIX * 25 * D
+
+
+def build_constants(nc, consts):
+    part_i = consts.tile([P, 1], I32, name="part_i")
+    nc.gpsimd.iota(part_i[:], pattern=[[0, 1]], base=0, channel_multiplier=1)
+    key_col_i = consts.tile([P, WIN], I32, name="key_col_i")
+    nc.gpsimd.iota(key_col_i[:], pattern=[[0, WIN // WIDTH], [1, WIDTH]], base=0, channel_multiplier=0)
+    key_row_i = consts.tile([P, WIN], I32, name="key_row_i")
+    nc.gpsimd.iota(key_row_i[:], pattern=[[1, WIN // WIDTH], [0, WIDTH]], base=0, channel_multiplier=0)
+
+    q_col_i = consts.tile([P, 1], I32, name="q_col_i")
+    nc.vector.tensor_scalar(out=q_col_i[:], in0=part_i[:], scalar1=WIDTH - 1, scalar2=None, op0=ALU.bitwise_and)
+    q_row_i = consts.tile([P, 1], I32, name="q_row_i")
+    nc.vector.tensor_scalar(
+        out=q_row_i[:], in0=part_i[:], scalar1=4, scalar2=1, op0=ALU.logical_shift_right, op1=ALU.bitwise_and
+    )
+    q_col = consts.tile([P, 1], F32, name="q_col")
+    nc.vector.tensor_copy(out=q_col[:], in_=q_col_i[:])
+    q_row = consts.tile([P, 1], F32, name="q_row")
+    nc.vector.tensor_scalar(out=q_row[:], in0=q_row_i[:], scalar1=2.0, scalar2=None, op0=ALU.add)
+
+    d_col = consts.tile([P, WIN], F32, name="d_col")
+    nc.vector.tensor_scalar(out=d_col[:], in0=key_col_i[:], scalar1=q_col[:, 0:1], scalar2=None, op0=ALU.subtract)
+    d_row = consts.tile([P, WIN], F32, name="d_row")
+    nc.vector.tensor_scalar(out=d_row[:], in0=key_row_i[:], scalar1=q_row[:, 0:1], scalar2=None, op0=ALU.subtract)
+    nc.vector.tensor_tensor(out=d_col[:], in0=d_col[:], in1=d_col[:], op=ALU.mult)
+    nc.vector.tensor_tensor(out=d_row[:], in0=d_row[:], in1=d_row[:], op=ALU.mult)
+    nc.vector.tensor_tensor(out=d_col[:], in0=d_col[:], in1=d_row[:], op=ALU.max)
+    bias = consts.tile([P, WIN], F32, name="bias")
+    nc.vector.tensor_scalar(out=bias[:], in0=d_col[:], scalar1=4.5, scalar2=FAR, op0=ALU.is_gt, op1=ALU.mult)
+
+    left = consts.tile([P, 1], F32, name="left")
+    nc.vector.tensor_scalar(out=left[:], in0=q_col[:], scalar1=-1.0, scalar2=2.0, op0=ALU.mult, op1=ALU.add)
+    right = consts.tile([P, 1], F32, name="right")
+    nc.vector.tensor_scalar(out=right[:], in0=q_col[:], scalar1=float(WIDTH - 3), scalar2=None, op0=ALU.subtract)
+    nc.vector.tensor_tensor(out=left[:], in0=left[:], in1=right[:], op=ALU.max)
+    n_out = consts.tile([P, 1], F32, name="n_out")
+    nc.vector.tensor_scalar(out=n_out[:], in0=left[:], scalar1=0.0, scalar2=5.0, op0=ALU.max, op1=ALU.mult)
+    edge = consts.tile([P, 1], F32, name="edge")
+    nc.vector.tensor_scalar(out=edge[:], in0=n_out[:], scalar1=0.5, scalar2=FAR, op0=ALU.is_lt, op1=ALU.mult)
+    return bias, n_out, edge
+
+
+def tile_relation_k_kernel(tc, x, w_qkv_words, w_qkv_scales, out):
+    nc = tc.nc
+    with ExitStack() as ctx:
+        keep = ctx.enter_context(tc.tile_pool(name="keep", bufs=1))
+        consts = ctx.enter_context(tc.tile_pool(name="consts", bufs=1))
+        x_stage = ctx.enter_context(tc.tile_pool(name="x_stage", bufs=3))
+        g_stage = ctx.enter_context(tc.tile_pool(name="g_stage", bufs=2))
+        w_stage = ctx.enter_context(tc.tile_pool(name="w_stage", bufs=4))
+        psum = ctx.enter_context(tc.psum_pool(name="psum", bufs=1))
+
+        x_view = x[0].rearrange("(g p t) h w -> p g (t h w)", p=P, t=PACK)
+        words = w_qkv_words.rearrange("g p n t -> g p (n t)").bitcast(I32).rearrange("g p n -> p g n")
+        scale_rows = w_qkv_scales.bitcast(I32).rearrange("(c k) (quad r) n -> quad r k c n", k=CHUNK, r=4)
+        out_view = out[0].rearrange("(j c) h w -> c j (h w)", c=P)
+
+        w_planes = keep.tile([P, NCHUNK, 3 * D], U8, name="w_planes", align_bytes=64)
+        nc.vector.memset(w_planes[:].bitcast(I32), 0)
+        for quad in range(4):
+            for r in range(4):
+                first = 32 * quad + r
+                nc.sync.dma_start(
+                    out=w_planes[:].bitcast(I32)[first : first + 4 * CHUNK : 4, :, :], in_=scale_rows[quad, r]
+                )
+
+        x_codes = keep.tile([P, PASSES, PIX], U32, name="x_codes", align_bytes=64)
+        x_planes = keep.tile([P, PASSES, PIX], U8, name="x_planes", align_bytes=64)
+        w_v = keep.tile([P, PASSES, D], U32, name="w_v", align_bytes=64)
+        q_diag = keep.tile([P, HALVES, NGRP, P], F32, name="q_diag")
+        v_diag = keep.tile([P, HALVES, NGRP, P], F32, name="v_diag")
+        k_pad = keep.tile([P, HALVES, (NGRP + 2) * GRP], F32, name="k_pad")
+        nc.vector.memset(q_diag[:], 0.0)
+        nc.vector.memset(k_pad[:], 0.0)
+        nc.vector.memset(v_diag[:], 0.0)
+        bias, n_out, edge = build_constants(nc, consts)
+
+        def load_x(c):
+            raw = x_stage.tile([P, CHUNK, PACK * PIX], BF16, name="raw")
+            nc.sync.dma_start(out=raw[:], in_=x_view[:, c * CHUNK : (c + 1) * CHUNK, :])
+            return raw
+
+        def quantise_x(c, raw):
+            grouped = g_stage.tile([P, CHUNK, PIX * PACK], BF16, name="grouped", align_bytes=64)
+            for i in range(CHUNK):
+                nc.vector.tensor_copy(
+                    out=grouped[:, i, :].rearrange("p (c i t) -> p c t i", i=4, t=PACK),
+                    in_=raw[:, i, :].rearrange("p (t c i) -> p c t i", t=PACK, i=4),
+                )
+            passes = slice(c * CHUNK, (c + 1) * CHUNK)
+            nc.vector.quantize_mx(
+                out=x_codes[:, passes, :].rearrange("p g w -> p (g w)").bitcast(FP8X4),
+                scales=x_planes[:, passes, :].rearrange("p g w -> p (g w)"),
+                in_=grouped[:].rearrange("p g e -> p (g e)"),
+            )
+
+        def mx_pass(acc, g, w_tile, w_cols, plane_cols):
+            chunk, k = divmod(g, CHUNK)
+            nc.tensor.matmul_mx(
+                out=acc,
+                lhsT=w_tile[:, w_cols].bitcast(FP8X4),
+                lhsT_scale=w_planes[4 * k : P, chunk, plane_cols],
+                rhs=x_codes[:, g, :].bitcast(FP8X4),
+                rhs_scale=x_planes[:, g, :],
+                start=(g == 0),
+                stop=(g == PASSES - 1),
+            )
+
+        qk_names = ["q0", "q1", "k0", "k1"]
+        qk_acc = [psum.tile([P, BANK], F32, name="acc_" + n, tag="bank_" + n) for n in qk_names]
+        raw_next = load_x(0)
+        for c in range(NCHUNK):
+            raw = raw_next
+            if c + 1 < NCHUNK:
+                raw_next = load_x(c + 1)
+            w_qk = w_stage.tile([P, CHUNK, 2 * D], U32, name="w_qk", align_bytes=64)
+            nc.sync.dma_start(out=w_qk[:].bitcast(I32), in_=words[:, c * CHUNK : (c + 1) * CHUNK, 0 : 2 * D])
+            quantise_x(c, raw)
+            for i in range(CHUNK):
+                for m in range(4):
+                    cols = slice(m * P, (m + 1) * P)
+                    mx_pass(qk_acc[m][:, 0:PIX], c * CHUNK + i, w_qk[:, i, :], cols, cols)
+
+        for c in range(NCHUNK):
+            passes = slice(c * CHUNK, (c + 1) * CHUNK)
+            nc.sync.dma_start(out=w_v[:, passes, :].bitcast(I32), in_=words[:, passes, 2 * D : 3 * D])
+
+        for j in range(HALVES):
+            for head in range(HEADS_T):
+                rows = slice(HD * head, HD * (head + 1))
+                copy = nc.vector.tensor_copy if head % 2 == 0 else nc.scalar.copy
+                copy(
+                    out=q_diag[rows, j, :, HD * head : HD * (head + 1)],
+                    in_=qk_acc[j][rows, 0:PIX].rearrange("p (i q) -> p i q", q=GRP),
+                )
+            copy = nc.vector.tensor_copy if j == 0 else nc.scalar.copy
+            copy(out=k_pad[:, j, GRP : GRP + PIX], in_=qk_acc[HALVES + j][:, 0:PIX])
+
+        n_tiles = HALVES * NGRP
+        masked = keep.tile([P, n_tiles, WIN], F32, name="masked")
+        expd = keep.tile([P, n_tiles, WIN], F32, name="expd")
+        att = keep.tile([P, n_tiles, WIN], F32, name="att", align_bytes=64)
+        att_t = keep.tile([P, n_tiles, WIN], F32, name="att_t", align_bytes=64)
+        top = keep.tile([P, n_tiles], F32, name="top")
+        neg_top = keep.tile([P, n_tiles], F32, name="neg_top")
+        in_sum = keep.tile([P, n_tiles], F32, name="in_sum")
+        out_exp = keep.tile([P, n_tiles], F32, name="out_exp")
+        total = keep.tile([P, n_tiles], F32, name="total")
+        inv = keep.tile([P, n_tiles], F32, name="inv")
+
+        s_tags = ["bank_s0", "bank_s1", "bank_q0", "bank_k0"]
+        for b in range(n_tiles // S_PER_BANK):
+            s_ps = psum.tile([P, S_PER_BANK, WIN], F32, name="s_ps", tag=s_tags[b])
+            tiles = slice(b * S_PER_BANK, (b + 1) * S_PER_BANK)
+            for a in range(S_PER_BANK):
+                j, i = divmod(b * S_PER_BANK + a, NGRP)
+                nc.tensor.matmul(
+                    out=s_ps[:, a, :],
+                    lhsT=q_diag[:, j, i, :],
+                    rhs=k_pad[:, j, GRP * i : GRP * i + WIN],
+                    start=True,
+                    stop=True,
+                )
+            nc.vector.tensor_tensor(
+                out=masked[:, tiles, :],
+                in0=s_ps[:],
+                in1=bias[:].unsqueeze(1).to_broadcast([P, S_PER_BANK, WIN]),
+                op=ALU.add,
+            )
+            nc.vector.tensor_reduce(out=top[:, tiles], in_=masked[:, tiles, :], axis=AXIS_X, op=ALU.max)
+            nc.vector.tensor_scalar(
+                out=neg_top[:, tiles], in0=top[:, tiles], scalar1=edge[:, 0:1], scalar2=-1.0, op0=ALU.max, op1=ALU.mult
+            )
+            for a in range(S_PER_BANK):
+                t = b * S_PER_BANK + a
+                nc.scalar.activation(
+                    out=expd[:, t, :],
+                    in_=masked[:, t, :],
+                    func=ACT.Exp,
+                    bias=neg_top[:, t : t + 1],
+                    scale=1.0,
+                    accum_out=in_sum[:, t : t + 1],
+                )
+            nc.scalar.activation(
+                out=out_exp[:, tiles], in_=neg_top[:, tiles], func=ACT.Exp, bias=edge[:, 0:1], scale=1.0
+            )
+            nc.vector.scalar_tensor_tensor(
+                out=total[:, tiles],
+                in0=out_exp[:, tiles],
+                scalar=n_out[:, 0:1],
+                in1=in_sum[:, tiles],
+                op0=ALU.mult,
+                op1=ALU.add,
+            )
+            nc.vector.reciprocal(out=inv[:, tiles], in_=total[:, tiles])
+            nc.vector.tensor_tensor(
+                out=att[:, tiles, :],
+                in0=expd[:, tiles, :],
+                in1=inv[:, tiles].unsqueeze(2).to_broadcast([P, S_PER_BANK, WIN]),
+                op=ALU.mult,
+            )
+        for j in range(HALVES):
+            tiles = slice(j * NGRP, (j + 1) * NGRP)
+            nc.vector.transpose(
+                out=att_t[:, tiles, :].rearrange("p t k -> p (t k)"), in_=att[:, tiles, :].rearrange("p t k -> p (t k)")
+            )
+
+        v_acc = [psum.tile([P, BANK], F32, name="acc_v%d" % j, tag="bank_v%d" % j) for j in range(HALVES)]
+        for g in range(PASSES):
+            for j in range(HALVES):
+                mx_pass(
+                    v_acc[j][:, 0:PIX], g, w_v[:, g, :], slice(j * P, (j + 1) * P), slice(2 * D + j * P, 2 * D + (j + 1) * P)
+                )
+
+        v_ct = keep.tile([P, HALVES, PIX], F32, name="v_ct", align_bytes=64)
+        v_kc = keep.tile([P, HALVES, PIX], F32, name="v_kc", align_bytes=64)
+        result = keep.tile([P, HALVES, PIX], F32, name="result")
+        o_tags = ["bank_q1", "bank_k1"]
+        order = [u for first in range(3) for u in range(first, NGRP, 3)]
+        for j in range(HALVES):
+            copy = nc.vector.tensor_copy if j == 0 else nc.scalar.copy
+            copy(out=v_ct[:, j, :], in_=v_acc[j][:, 0:PIX])
+            nc.vector.transpose(out=v_kc[:, j, :], in_=v_ct[:, j, :])
+            for head in range(HEADS_T):
+                rows = slice(HD * head, HD * (head + 1))
+                copy = nc.vector.tensor_copy if head % 2 == 0 else nc.scalar.copy
+                copy(
+                    out=v_diag[rows, j, :, HD * head : HD * (head + 1)],
+                    in_=v_kc[rows, j, :].rearrange("p (u c) -> p u c", c=HD),
+                )
+            o_ps = psum.tile([P, BANK], F32, name="o_ps", tag=o_tags[j])
+            att_j = att_t[:, j * NGRP : (j + 1) * NGRP, :].rearrange("p t k -> p (t k)")
+            for n, u in enumerate(order):
+                lo = max(u - 1, 0)
+                hi = min(u + 1, NGRP - 1)
+                count = hi - lo + 1
+                start_col = WIN * lo + GRP * (u - lo + 1)
+                nc.tensor.matmul(
+                    out=o_ps[:, GRP * lo : GRP * (hi + 1)].rearrange("p (d q) -> p d q", q=GRP),
+                    lhsT=v_diag[:, j, u, :],
+                    rhs=att_j[:, start_col : start_col + 2 * GRP * count].rearrange("p (d w) -> p d w", w=2 * GRP)[
+                        :, :, 0:GRP
+                    ],
+                    start=(n == 0),
+                    stop=(n == NGRP - 1),
+                )
+            copy = nc.vector.tensor_copy if j == 0 else nc.scalar.copy
+            copy(out=result[:, j, :], in_=o_ps[:, 0:PIX])
+            nc.sync.dma_start(out=out_view[:, j, :], in_=result[:, j, :])

@@ -78,6 +78,7 @@ def build_constants(nc, consts):
 def tile_relation_k_kernel(tc, x, w_qkv_words, w_qkv_scales, out):
     nc = tc.nc
     with ExitStack() as ctx:
+        ctx.enter_context(tc.manual_schedule())
         keep = ctx.enter_context(tc.tile_pool(name="keep", bufs=1))
         consts = ctx.enter_context(tc.tile_pool(name="consts", bufs=1))
         x_stage = ctx.enter_context(tc.tile_pool(name="x_stage", bufs=3))
@@ -105,23 +106,23 @@ def tile_relation_k_kernel(tc, x, w_qkv_words, w_qkv_scales, out):
         q_diag = keep.tile([P, HALVES, NGRP, P], F32, name="q_diag")
         v_diag = keep.tile([P, HALVES, NGRP, P], F32, name="v_diag")
         k_pad = keep.tile([P, HALVES, (NGRP + 2) * GRP], F32, name="k_pad")
-        nc.vector.memset(q_diag[:], 0.0)
-        nc.vector.memset(k_pad[:], 0.0)
-        nc.vector.memset(v_diag[:], 0.0)
-        bias, n_out, edge = build_constants(nc, consts)
 
         def load_x(c):
             raw = x_stage.tile([P, CHUNK, PACK * PIX], BF16, name="raw")
             nc.sync.dma_start(out=raw[:], in_=x_view[:, c * CHUNK : (c + 1) * CHUNK, :])
             return raw
 
-        def quantise_x(c, raw):
+        def regroup_x(raw):
             grouped = g_stage.tile([P, CHUNK, PIX * PACK], BF16, name="grouped", align_bytes=64)
             for i in range(CHUNK):
-                nc.vector.tensor_copy(
+                copy = nc.scalar.copy if i == CHUNK - 1 else nc.vector.tensor_copy
+                copy(
                     out=grouped[:, i, :].rearrange("p (c i t) -> p c t i", i=4, t=PACK),
                     in_=raw[:, i, :].rearrange("p (t c i) -> p c t i", t=PACK, i=4),
                 )
+            return grouped
+
+        def quantise_x(c, grouped):
             passes = slice(c * CHUNK, (c + 1) * CHUNK)
             nc.vector.quantize_mx(
                 out=x_codes[:, passes, :].rearrange("p g w -> p (g w)").bitcast(FP8X4),
@@ -143,14 +144,24 @@ def tile_relation_k_kernel(tc, x, w_qkv_words, w_qkv_scales, out):
 
         qk_names = ["q0", "q1", "k0", "k1"]
         qk_acc = [psum.tile([P, BANK], F32, name="acc_" + n, tag="bank_" + n) for n in qk_names]
-        raw_next = load_x(0)
+        raws = [load_x(0), load_x(1)]
+        grouped_next = regroup_x(raws[0])
         for c in range(NCHUNK):
-            raw = raw_next
-            if c + 1 < NCHUNK:
-                raw_next = load_x(c + 1)
             w_qk = w_stage.tile([P, CHUNK, 2 * D], U32, name="w_qk", align_bytes=64)
             nc.sync.dma_start(out=w_qk[:].bitcast(I32), in_=words[:, c * CHUNK : (c + 1) * CHUNK, 0 : 2 * D])
-            quantise_x(c, raw)
+            if c + 2 < NCHUNK:
+                raws.append(load_x(c + 2))
+            grouped = grouped_next
+            if c + 1 < NCHUNK:
+                grouped_next = regroup_x(raws[c + 1])
+            quantise_x(c, grouped)
+            if c == 0:
+                nc.vector.memset(q_diag[:], 0.0)
+                nc.vector.memset(k_pad[:], 0.0)
+                nc.vector.memset(v_diag[:], 0.0)
+                bias, n_out, edge = build_constants(nc, consts)
+                warm = consts.tile([P, 1], F32, name="warm")
+                nc.scalar.activation(out=warm[:], in_=n_out[:], func=ACT.Exp)
             for i in range(CHUNK):
                 for m in range(4):
                     cols = slice(m * P, (m + 1) * P)
@@ -160,6 +171,33 @@ def tile_relation_k_kernel(tc, x, w_qkv_words, w_qkv_scales, out):
             passes = slice(c * CHUNK, (c + 1) * CHUNK)
             nc.sync.dma_start(out=w_v[:, passes, :].bitcast(I32), in_=words[:, passes, 2 * D : 3 * D])
 
+        v_acc = [psum.tile([P, BANK], F32, name="acc_v%d" % j, tag="bank_v%d" % j) for j in range(HALVES)]
+
+        def v_passes(c):
+            for j in range(HALVES):
+                for g in range(c * CHUNK, (c + 1) * CHUNK):
+                    mx_pass(
+                        v_acc[j][:, 0:PIX],
+                        g,
+                        w_v[:, g, :],
+                        slice(j * P, (j + 1) * P),
+                        slice(2 * D + j * P, 2 * D + (j + 1) * P),
+                    )
+
+        n_tiles = HALVES * NGRP
+        masked = keep.tile([P, n_tiles, WIN], F32, name="masked")
+        expd = keep.tile([P, n_tiles, WIN], F32, name="expd", align_bytes=64)
+        expd_t = keep.tile([P, n_tiles, WIN], F32, name="expd_t", align_bytes=64)
+        top = keep.tile([P, n_tiles], F32, name="top")
+        neg_top = keep.tile([P, n_tiles], F32, name="neg_top")
+        in_sum = keep.tile([P, n_tiles], F32, name="in_sum")
+        out_exp = keep.tile([P, n_tiles], F32, name="out_exp")
+        total = keep.tile([P, n_tiles], F32, name="total")
+        inv = keep.tile([P, n_tiles], F32, name="inv")
+        inv_wide = keep.tile([P, n_tiles, HD], F32, name="inv_wide", align_bytes=64)
+        inv_t = keep.tile([P, n_tiles, GRP], F32, name="inv_t", align_bytes=64)
+
+        v_passes(0)
         for j in range(HALVES):
             for head in range(HEADS_T):
                 rows = slice(HD * head, HD * (head + 1))
@@ -171,22 +209,11 @@ def tile_relation_k_kernel(tc, x, w_qkv_words, w_qkv_scales, out):
             copy = nc.vector.tensor_copy if j == 0 else nc.scalar.copy
             copy(out=k_pad[:, j, GRP : GRP + PIX], in_=qk_acc[HALVES + j][:, 0:PIX])
 
-        n_tiles = HALVES * NGRP
-        masked = keep.tile([P, n_tiles, WIN], F32, name="masked")
-        expd = keep.tile([P, n_tiles, WIN], F32, name="expd")
-        att = keep.tile([P, n_tiles, WIN], F32, name="att", align_bytes=64)
-        att_t = keep.tile([P, n_tiles, WIN], F32, name="att_t", align_bytes=64)
-        top = keep.tile([P, n_tiles], F32, name="top")
-        neg_top = keep.tile([P, n_tiles], F32, name="neg_top")
-        in_sum = keep.tile([P, n_tiles], F32, name="in_sum")
-        out_exp = keep.tile([P, n_tiles], F32, name="out_exp")
-        total = keep.tile([P, n_tiles], F32, name="total")
-        inv = keep.tile([P, n_tiles], F32, name="inv")
-
         s_tags = ["bank_s0", "bank_s1", "bank_q0", "bank_k0"]
+        s_banks = []
         for b in range(n_tiles // S_PER_BANK):
-            s_ps = psum.tile([P, S_PER_BANK, WIN], F32, name="s_ps", tag=s_tags[b])
-            tiles = slice(b * S_PER_BANK, (b + 1) * S_PER_BANK)
+            s_ps = psum.tile([P, S_PER_BANK, WIN], F32, name="s_ps%d" % b, tag=s_tags[b])
+            s_banks.append(s_ps)
             for a in range(S_PER_BANK):
                 j, i = divmod(b * S_PER_BANK + a, NGRP)
                 nc.tensor.matmul(
@@ -196,9 +223,16 @@ def tile_relation_k_kernel(tc, x, w_qkv_words, w_qkv_scales, out):
                     start=True,
                     stop=True,
                 )
+            if b == 1:
+                v_passes(1)
+        for c in range(2, NCHUNK):
+            v_passes(c)
+
+        for b in range(n_tiles // S_PER_BANK):
+            tiles = slice(b * S_PER_BANK, (b + 1) * S_PER_BANK)
             nc.vector.tensor_tensor(
                 out=masked[:, tiles, :],
-                in0=s_ps[:],
+                in0=s_banks[b][:],
                 in1=bias[:].unsqueeze(1).to_broadcast([P, S_PER_BANK, WIN]),
                 op=ALU.add,
             )
@@ -216,46 +250,26 @@ def tile_relation_k_kernel(tc, x, w_qkv_words, w_qkv_scales, out):
                     scale=1.0,
                     accum_out=in_sum[:, t : t + 1],
                 )
-            nc.scalar.activation(
-                out=out_exp[:, tiles], in_=neg_top[:, tiles], func=ACT.Exp, bias=edge[:, 0:1], scale=1.0
-            )
-            nc.vector.scalar_tensor_tensor(
-                out=total[:, tiles],
-                in0=out_exp[:, tiles],
-                scalar=n_out[:, 0:1],
-                in1=in_sum[:, tiles],
-                op0=ALU.mult,
-                op1=ALU.add,
-            )
-            nc.vector.reciprocal(out=inv[:, tiles], in_=total[:, tiles])
-            nc.vector.tensor_tensor(
-                out=att[:, tiles, :],
-                in0=expd[:, tiles, :],
-                in1=inv[:, tiles].unsqueeze(2).to_broadcast([P, S_PER_BANK, WIN]),
-                op=ALU.mult,
-            )
+        nc.scalar.activation(out=out_exp[:], in_=neg_top[:], func=ACT.Exp, bias=edge[:, 0:1], scale=1.0)
+
         for j in range(HALVES):
             tiles = slice(j * NGRP, (j + 1) * NGRP)
             nc.vector.transpose(
-                out=att_t[:, tiles, :].rearrange("p t k -> p (t k)"), in_=att[:, tiles, :].rearrange("p t k -> p (t k)")
+                out=expd_t[:, tiles, :].rearrange("p t k -> p (t k)"), in_=expd[:, tiles, :].rearrange("p t k -> p (t k)")
             )
+        nc.vector.scalar_tensor_tensor(
+            out=total[:], in0=out_exp[:], scalar=n_out[:, 0:1], in1=in_sum[:], op0=ALU.mult, op1=ALU.add
+        )
+        nc.vector.reciprocal(out=inv[:], in_=total[:])
+        nc.vector.tensor_copy(out=inv_wide[:], in_=inv[:].unsqueeze(2).to_broadcast([P, n_tiles, HD]))
+        nc.vector.transpose(out=inv_t[:].rearrange("p t q -> p (t q)"), in_=inv_wide[:].rearrange("p t c -> p (t c)"))
 
-        v_acc = [psum.tile([P, BANK], F32, name="acc_v%d" % j, tag="bank_v%d" % j) for j in range(HALVES)]
-        for g in range(PASSES):
-            for j in range(HALVES):
-                mx_pass(
-                    v_acc[j][:, 0:PIX], g, w_v[:, g, :], slice(j * P, (j + 1) * P), slice(2 * D + j * P, 2 * D + (j + 1) * P)
-                )
-
-        v_ct = keep.tile([P, HALVES, PIX], F32, name="v_ct", align_bytes=64)
         v_kc = keep.tile([P, HALVES, PIX], F32, name="v_kc", align_bytes=64)
         result = keep.tile([P, HALVES, PIX], F32, name="result")
-        o_tags = ["bank_q1", "bank_k1"]
-        order = [u for first in range(3) for u in range(first, NGRP, 3)]
         for j in range(HALVES):
-            copy = nc.vector.tensor_copy if j == 0 else nc.scalar.copy
-            copy(out=v_ct[:, j, :], in_=v_acc[j][:, 0:PIX])
-            nc.vector.transpose(out=v_kc[:, j, :], in_=v_ct[:, j, :])
+            for half in range(2):
+                cols = slice(half * P, (half + 1) * P)
+                nc.vector.transpose(out=v_kc[:, j, cols], in_=v_acc[j][:, cols])
             for head in range(HEADS_T):
                 rows = slice(HD * head, HD * (head + 1))
                 copy = nc.vector.tensor_copy if head % 2 == 0 else nc.scalar.copy
@@ -263,8 +277,11 @@ def tile_relation_k_kernel(tc, x, w_qkv_words, w_qkv_scales, out):
                     out=v_diag[rows, j, :, HD * head : HD * (head + 1)],
                     in_=v_kc[rows, j, :].rearrange("p (u c) -> p u c", c=HD),
                 )
-            o_ps = psum.tile([P, BANK], F32, name="o_ps", tag=o_tags[j])
-            att_j = att_t[:, j * NGRP : (j + 1) * NGRP, :].rearrange("p t k -> p (t k)")
+        o_tags = ["bank_q1", "bank_k1"]
+        order = [u for first in range(3) for u in range(first, NGRP, 3)]
+        for j in range(HALVES):
+            o_ps = psum.tile([P, BANK], F32, name="o_ps%d" % j, tag=o_tags[j])
+            exp_j = expd_t[:, j * NGRP : (j + 1) * NGRP, :].rearrange("p t k -> p (t k)")
             for n, u in enumerate(order):
                 lo = max(u - 1, 0)
                 hi = min(u + 1, NGRP - 1)
@@ -273,12 +290,16 @@ def tile_relation_k_kernel(tc, x, w_qkv_words, w_qkv_scales, out):
                 nc.tensor.matmul(
                     out=o_ps[:, GRP * lo : GRP * (hi + 1)].rearrange("p (d q) -> p d q", q=GRP),
                     lhsT=v_diag[:, j, u, :],
-                    rhs=att_j[:, start_col : start_col + 2 * GRP * count].rearrange("p (d w) -> p d w", w=2 * GRP)[
+                    rhs=exp_j[:, start_col : start_col + 2 * GRP * count].rearrange("p (d w) -> p d w", w=2 * GRP)[
                         :, :, 0:GRP
                     ],
                     start=(n == 0),
                     stop=(n == NGRP - 1),
                 )
-            copy = nc.vector.tensor_copy if j == 0 else nc.scalar.copy
-            copy(out=result[:, j, :], in_=o_ps[:, 0:PIX])
+            nc.vector.tensor_tensor(
+                out=result[:, j, :],
+                in0=o_ps[:, 0:PIX],
+                in1=inv_t[:, j * NGRP : (j + 1) * NGRP, :].rearrange("p t q -> p (t q)"),
+                op=ALU.mult,
+            )
             nc.sync.dma_start(out=out_view[:, j, :], in_=result[:, j, :])

@@ -81,7 +81,7 @@ def tile_relation_k_kernel(tc, x, w_qkv_words, w_qkv_scales, out):
         ctx.enter_context(tc.manual_schedule())
         keep = ctx.enter_context(tc.tile_pool(name="keep", bufs=1))
         consts = ctx.enter_context(tc.tile_pool(name="consts", bufs=1))
-        x_stage = ctx.enter_context(tc.tile_pool(name="x_stage", bufs=3))
+        x_stage = ctx.enter_context(tc.tile_pool(name="x_stage", bufs=4))
         g_stage = ctx.enter_context(tc.tile_pool(name="g_stage", bufs=2))
         w_stage = ctx.enter_context(tc.tile_pool(name="w_stage", bufs=4))
         psum = ctx.enter_context(tc.psum_pool(name="psum", bufs=1))
@@ -93,7 +93,8 @@ def tile_relation_k_kernel(tc, x, w_qkv_words, w_qkv_scales, out):
 
         w_planes = keep.tile([P, NCHUNK, 3 * D], U8, name="w_planes", align_bytes=64)
         nc.vector.memset(w_planes[:].bitcast(I32), 0)
-        for quad in range(4):
+
+        def load_scales(quad):
             for r in range(4):
                 first = 32 * quad + r
                 nc.sync.dma_start(
@@ -111,6 +112,11 @@ def tile_relation_k_kernel(tc, x, w_qkv_words, w_qkv_scales, out):
             raw = x_stage.tile([P, CHUNK, PACK * PIX], BF16, name="raw")
             nc.sync.dma_start(out=raw[:], in_=x_view[:, c * CHUNK : (c + 1) * CHUNK, :])
             return raw
+
+        def load_w_qk(c):
+            w_qk = w_stage.tile([P, CHUNK, 2 * D], U32, name="w_qk", align_bytes=64)
+            nc.sync.dma_start(out=w_qk[:].bitcast(I32), in_=words[:, c * CHUNK : (c + 1) * CHUNK, 0 : 2 * D])
+            return w_qk
 
         def regroup_x(raw):
             grouped = g_stage.tile([P, CHUNK, PIX * PACK], BF16, name="grouped", align_bytes=64)
@@ -144,13 +150,22 @@ def tile_relation_k_kernel(tc, x, w_qkv_words, w_qkv_scales, out):
 
         qk_names = ["q0", "q1", "k0", "k1"]
         qk_acc = [psum.tile([P, BANK], F32, name="acc_" + n, tag="bank_" + n) for n in qk_names]
-        raws = [load_x(0), load_x(1)]
+        raws = [load_x(0)]
+        load_scales(0)
+        raws.append(load_x(1))
+        load_scales(1)
+        w_qks = [load_w_qk(0)]
+        load_scales(2)
+        raws.append(load_x(2))
+        w_qks.append(load_w_qk(1))
+        load_scales(3)
         grouped_next = regroup_x(raws[0])
         for c in range(NCHUNK):
-            w_qk = w_stage.tile([P, CHUNK, 2 * D], U32, name="w_qk", align_bytes=64)
-            nc.sync.dma_start(out=w_qk[:].bitcast(I32), in_=words[:, c * CHUNK : (c + 1) * CHUNK, 0 : 2 * D])
+            if c + 3 < NCHUNK:
+                raws.append(load_x(c + 3))
             if c + 2 < NCHUNK:
-                raws.append(load_x(c + 2))
+                w_qks.append(load_w_qk(c + 2))
+            w_qk = w_qks[c]
             grouped = grouped_next
             if c + 1 < NCHUNK:
                 grouped_next = regroup_x(raws[c + 1])

@@ -83,22 +83,21 @@ def tile_relation_k_kernel(tc, x, w_qkv_words, w_qkv_scales, out):
         consts = ctx.enter_context(tc.tile_pool(name="consts", bufs=1))
         x_stage = ctx.enter_context(tc.tile_pool(name="x_stage", bufs=4))
         g_stage = ctx.enter_context(tc.tile_pool(name="g_stage", bufs=2))
-        w_stage = ctx.enter_context(tc.tile_pool(name="w_stage", bufs=4))
+        w_stage = ctx.enter_context(tc.tile_pool(name="w_stage", bufs=6))
         psum = ctx.enter_context(tc.psum_pool(name="psum", bufs=1))
 
         x_view = x[0].rearrange("(g p t) h w -> p g (t h w)", p=P, t=PACK)
         words = w_qkv_words.rearrange("g p n t -> g p (n t)").bitcast(I32).rearrange("g p n -> p g n")
-        scale_rows = w_qkv_scales.bitcast(I32).rearrange("(c k) (quad r) n -> quad r k c n", k=CHUNK, r=4)
+        scale_rows = w_qkv_scales.bitcast(F32).rearrange("(c k) (quad r) n -> quad r k c n", k=CHUNK, r=4)
         out_view = out[0].rearrange("(j c) h w -> c j (h w)", c=P)
 
         w_planes = keep.tile([P, NCHUNK, 3 * D], U8, name="w_planes", align_bytes=64)
         nc.vector.memset(w_planes[:].bitcast(I32), 0)
-
-        def load_scales(quad):
+        for quad in range(4):
             for r in range(4):
                 first = 32 * quad + r
-                nc.sync.dma_start(
-                    out=w_planes[:].bitcast(I32)[first : first + 4 * CHUNK : 4, :, :], in_=scale_rows[quad, r]
+                nc.gpsimd.dma_start(
+                    out=w_planes[:].bitcast(F32)[first : first + 4 * CHUNK : 4, :, :], in_=scale_rows[quad, r]
                 )
 
         x_codes = keep.tile([P, PASSES, PIX], U32, name="x_codes", align_bytes=64)
@@ -121,7 +120,7 @@ def tile_relation_k_kernel(tc, x, w_qkv_words, w_qkv_scales, out):
         def regroup_x(raw):
             grouped = g_stage.tile([P, CHUNK, PIX * PACK], BF16, name="grouped", align_bytes=64)
             for i in range(CHUNK):
-                copy = nc.scalar.copy if i == CHUNK - 1 else nc.vector.tensor_copy
+                copy = nc.vector.tensor_copy if i % 2 == 0 else nc.scalar.copy
                 copy(
                     out=grouped[:, i, :].rearrange("p (c i t) -> p c t i", i=4, t=PACK),
                     in_=raw[:, i, :].rearrange("p (t c i) -> p c t i", t=PACK, i=4),
@@ -150,15 +149,10 @@ def tile_relation_k_kernel(tc, x, w_qkv_words, w_qkv_scales, out):
 
         qk_names = ["q0", "q1", "k0", "k1"]
         qk_acc = [psum.tile([P, BANK], F32, name="acc_" + n, tag="bank_" + n) for n in qk_names]
-        raws = [load_x(0)]
-        load_scales(0)
-        raws.append(load_x(1))
-        load_scales(1)
+        raws = [load_x(0), load_x(1)]
         w_qks = [load_w_qk(0)]
-        load_scales(2)
         raws.append(load_x(2))
         w_qks.append(load_w_qk(1))
-        load_scales(3)
         grouped_next = regroup_x(raws[0])
         for c in range(NCHUNK):
             if c + 3 < NCHUNK:
@@ -170,7 +164,7 @@ def tile_relation_k_kernel(tc, x, w_qkv_words, w_qkv_scales, out):
             if c + 1 < NCHUNK:
                 grouped_next = regroup_x(raws[c + 1])
             quantise_x(c, grouped)
-            if c == 0:
+            if c == NCHUNK // 2:
                 nc.vector.memset(q_diag[:], 0.0)
                 nc.vector.memset(k_pad[:], 0.0)
                 nc.vector.memset(v_diag[:], 0.0)

@@ -1,6 +1,7 @@
 from contextlib import ExitStack
 
 import concourse.mybir as mybir
+from concourse.masks import make_identity
 
 F32 = mybir.dt.float32
 BF16 = mybir.dt.bfloat16
@@ -60,8 +61,15 @@ def build_constants(nc, consts):
     nc.vector.tensor_tensor(out=d_col[:], in0=d_col[:], in1=d_col[:], op=ALU.mult)
     nc.vector.tensor_tensor(out=d_row[:], in0=d_row[:], in1=d_row[:], op=ALU.mult)
     nc.vector.tensor_tensor(out=d_col[:], in0=d_col[:], in1=d_row[:], op=ALU.max)
-    bias = consts.tile([P, WIN], F32, name="bias")
-    nc.vector.tensor_scalar(out=bias[:], in0=d_col[:], scalar1=4.5, scalar2=FAR, op0=ALU.is_gt, op1=ALU.mult)
+    bias = consts.tile([P, S_PER_BANK, WIN], BF16, name="bias")
+    nc.vector.tensor_scalar(
+        out=bias[:],
+        in0=d_col[:].unsqueeze(1).to_broadcast([P, S_PER_BANK, WIN]),
+        scalar1=4.5,
+        scalar2=FAR,
+        op0=ALU.is_gt,
+        op1=ALU.mult,
+    )
 
     left = consts.tile([P, 1], F32, name="left")
     nc.vector.tensor_scalar(out=left[:], in0=q_col[:], scalar1=-1.0, scalar2=2.0, op0=ALU.mult, op1=ALU.add)
@@ -169,18 +177,33 @@ def tile_relation_k_kernel(tc, x, w_qkv_words, w_qkv_scales, out):
                 nc.vector.memset(k_pad[:], 0.0)
                 nc.vector.memset(v_diag[:], 0.0)
                 bias, n_out, edge = build_constants(nc, consts)
+                ident = consts.tile([P, P], BF16, name="ident")
+                make_identity(nc, ident[:])
                 warm = consts.tile([P, 1], F32, name="warm")
                 nc.scalar.activation(out=warm[:], in_=n_out[:], func=ACT.Exp)
-            for i in range(CHUNK):
-                for m in range(4):
-                    cols = slice(m * P, (m + 1) * P)
-                    mx_pass(qk_acc[m][:, 0:PIX], c * CHUNK + i, w_qk[:, i, :], cols, cols)
+            if c == NCHUNK - 1:
+                order = [(i, m) for m in range(4) for i in range(CHUNK)]
+            else:
+                order = [(i, m) for i in range(CHUNK) for m in range(4)]
+            for i, m in order:
+                cols = slice(m * P, (m + 1) * P)
+                mx_pass(qk_acc[m][:, 0:PIX], c * CHUNK + i, w_qk[:, i, :], cols, cols)
+            if c == NCHUNK // 2 + 1:
+                s_banks = []
+                for b in range(HALVES * NGRP // S_PER_BANK):
+                    s_ps = psum.tile([P, S_PER_BANK, WIN], F32, name="s_ps%d" % b, tag="bank_s%d" % b)
+                    s_banks.append(s_ps)
+                    nc.tensor.matmul(
+                        out=s_ps[:].rearrange("p a k -> p (a k)"),
+                        lhsT=ident[:],
+                        rhs=bias[:].rearrange("p a k -> p (a k)"),
+                        start=True,
+                        stop=False,
+                    )
 
         for c in range(NCHUNK):
             passes = slice(c * CHUNK, (c + 1) * CHUNK)
             nc.sync.dma_start(out=w_v[:, passes, :].bitcast(I32), in_=words[:, passes, 2 * D : 3 * D])
-
-        v_acc = [psum.tile([P, BANK], F32, name="acc_v%d" % j, tag="bank_v%d" % j) for j in range(HALVES)]
 
         def v_passes(c):
             for j in range(HALVES):
@@ -194,7 +217,6 @@ def tile_relation_k_kernel(tc, x, w_qkv_words, w_qkv_scales, out):
                     )
 
         n_tiles = HALVES * NGRP
-        masked = keep.tile([P, n_tiles, WIN], F32, name="masked")
         expd = keep.tile([P, n_tiles, WIN], F32, name="expd", align_bytes=64)
         expd_t = keep.tile([P, n_tiles, WIN], F32, name="expd_t", align_bytes=64)
         top = keep.tile([P, n_tiles], F32, name="top")
@@ -206,46 +228,34 @@ def tile_relation_k_kernel(tc, x, w_qkv_words, w_qkv_scales, out):
         inv_wide = keep.tile([P, n_tiles, HD], F32, name="inv_wide", align_bytes=64)
         inv_t = keep.tile([P, n_tiles, GRP], F32, name="inv_t", align_bytes=64)
 
-        v_passes(0)
-        for j in range(HALVES):
+        for j, copy in enumerate([nc.vector.tensor_copy, nc.scalar.copy]):
             for head in range(HEADS_T):
                 rows = slice(HD * head, HD * (head + 1))
-                copy = nc.vector.tensor_copy if head % 2 == 0 else nc.scalar.copy
                 copy(
                     out=q_diag[rows, j, :, HD * head : HD * (head + 1)],
                     in_=qk_acc[j][rows, 0:PIX].rearrange("p (i q) -> p i q", q=GRP),
                 )
-            copy = nc.vector.tensor_copy if j == 0 else nc.scalar.copy
             copy(out=k_pad[:, j, GRP : GRP + PIX], in_=qk_acc[HALVES + j][:, 0:PIX])
 
-        s_tags = ["bank_s0", "bank_s1", "bank_q0", "bank_k0"]
-        s_banks = []
-        for b in range(n_tiles // S_PER_BANK):
-            s_ps = psum.tile([P, S_PER_BANK, WIN], F32, name="s_ps%d" % b, tag=s_tags[b])
-            s_banks.append(s_ps)
-            for a in range(S_PER_BANK):
-                j, i = divmod(b * S_PER_BANK + a, NGRP)
-                nc.tensor.matmul(
-                    out=s_ps[:, a, :],
-                    lhsT=q_diag[:, j, i, :],
-                    rhs=k_pad[:, j, GRP * i : GRP * i + WIN],
-                    start=True,
-                    stop=True,
-                )
-            if b == 1:
-                v_passes(1)
-        for c in range(2, NCHUNK):
+        for t in range(n_tiles):
+            j, i = divmod(t, NGRP)
+            b, a = divmod(t, S_PER_BANK)
+            nc.tensor.matmul(
+                out=s_banks[b][:, a, :],
+                lhsT=q_diag[:, j, i, :],
+                rhs=k_pad[:, j, GRP * i : GRP * i + WIN],
+                start=False,
+                stop=(a == S_PER_BANK - 1),
+            )
+
+        v_tags = ["bank_q0", "bank_k0"]
+        v_acc = [psum.tile([P, BANK], F32, name="acc_v%d" % j, tag=v_tags[j]) for j in range(HALVES)]
+        for c in range(NCHUNK):
             v_passes(c)
 
         for b in range(n_tiles // S_PER_BANK):
             tiles = slice(b * S_PER_BANK, (b + 1) * S_PER_BANK)
-            nc.vector.tensor_tensor(
-                out=masked[:, tiles, :],
-                in0=s_banks[b][:],
-                in1=bias[:].unsqueeze(1).to_broadcast([P, S_PER_BANK, WIN]),
-                op=ALU.add,
-            )
-            nc.vector.tensor_reduce(out=top[:, tiles], in_=masked[:, tiles, :], axis=AXIS_X, op=ALU.max)
+            nc.vector.tensor_reduce(out=top[:, tiles], in_=s_banks[b][:], axis=AXIS_X, op=ALU.max)
             nc.vector.tensor_scalar(
                 out=neg_top[:, tiles], in0=top[:, tiles], scalar1=edge[:, 0:1], scalar2=-1.0, op0=ALU.max, op1=ALU.mult
             )
@@ -253,7 +263,7 @@ def tile_relation_k_kernel(tc, x, w_qkv_words, w_qkv_scales, out):
                 t = b * S_PER_BANK + a
                 nc.scalar.activation(
                     out=expd[:, t, :],
-                    in_=masked[:, t, :],
+                    in_=s_banks[b][:, a, :],
                     func=ACT.Exp,
                     bias=neg_top[:, t : t + 1],
                     scale=1.0,

@@ -28,6 +28,8 @@ NGRP = PIX // GRP
 WIN = 3 * GRP
 CHUNK = 4
 NCHUNK = PASSES // CHUNK
+SLOT = 8
+NSLOT = PASSES // SLOT
 BANK = 512
 S_PER_BANK = 4
 FAR = -1.0e30
@@ -96,17 +98,25 @@ def tile_relation_k_kernel(tc, x, w_qkv_words, w_qkv_scales, out):
 
         x_view = x[0].rearrange("(g p t) h w -> p g (t h w)", p=P, t=PACK)
         words = w_qkv_words.rearrange("g p n t -> g p (n t)").bitcast(I32).rearrange("g p n -> p g n")
-        scale_rows = w_qkv_scales.bitcast(F32).rearrange("(c k) (quad r) n -> quad r k c n", k=CHUNK, r=4)
+        scale_rows = w_qkv_scales.bitcast(F32).rearrange("(s g) (quad r) n -> s r quad g n", g=SLOT, r=4)
         out_view = out[0].rearrange("(j c) h w -> c j (h w)", c=P)
 
-        w_planes = keep.tile([P, NCHUNK, 3 * D], U8, name="w_planes", align_bytes=64)
-        nc.vector.memset(w_planes[:].bitcast(I32), 0)
-        for quad in range(4):
+        w_planes = keep.tile([P, PASSES, 3 * D], U8, name="w_planes", align_bytes=64)
+
+        def clear_planes(s):
+            nc.vector.memset(w_planes[:, s * SLOT : (s + 1) * SLOT, :].bitcast(I32), 0)
+
+        def load_scales(s):
             for r in range(4):
-                first = 32 * quad + r
                 nc.gpsimd.dma_start(
-                    out=w_planes[:].bitcast(F32)[first : first + 4 * CHUNK : 4, :, :], in_=scale_rows[quad, r]
+                    out=w_planes[:].bitcast(F32)[4 * s + r : P : GRP, s * SLOT : (s + 1) * SLOT, :],
+                    in_=scale_rows[s, r],
                 )
+
+        clear_planes(0)
+        load_scales(0)
+        clear_planes(1)
+        load_scales(1)
 
         x_codes = keep.tile([P, PASSES, PIX], U32, name="x_codes", align_bytes=64)
         x_planes = keep.tile([P, PASSES, PIX], U8, name="x_planes", align_bytes=64)
@@ -144,11 +154,10 @@ def tile_relation_k_kernel(tc, x, w_qkv_words, w_qkv_scales, out):
             )
 
         def mx_pass(acc, g, w_tile, w_cols, plane_cols):
-            chunk, k = divmod(g, CHUNK)
             nc.tensor.matmul_mx(
                 out=acc,
                 lhsT=w_tile[:, w_cols].bitcast(FP8X4),
-                lhsT_scale=w_planes[4 * k : P, chunk, plane_cols],
+                lhsT_scale=w_planes[4 * (g // SLOT) : P, g, plane_cols],
                 rhs=x_codes[:, g, :].bitcast(FP8X4),
                 rhs_scale=x_planes[:, g, :],
                 start=(g == 0),
@@ -172,6 +181,9 @@ def tile_relation_k_kernel(tc, x, w_qkv_words, w_qkv_scales, out):
             if c + 1 < NCHUNK:
                 grouped_next = regroup_x(raws[c + 1])
             quantise_x(c, grouped)
+            if c + 2 < NSLOT:
+                clear_planes(c + 2)
+                load_scales(c + 2)
             if c == NCHUNK // 2:
                 nc.vector.memset(q_diag[:], 0.0)
                 nc.vector.memset(k_pad[:], 0.0)

@@ -26,10 +26,13 @@ HD = 32
 GRP = 32
 NGRP = PIX // GRP
 WIN = 3 * GRP
-CHUNK = 4
+CHUNK = 2
 NCHUNK = PASSES // CHUNK
 SLOT = 8
 NSLOT = PASSES // SLOT
+V_CHUNK = 4
+X_LEAD = 6
+W_LEAD = 5
 BANK = 512
 S_PER_BANK = 4
 FAR = -1.0e30
@@ -91,9 +94,9 @@ def tile_relation_k_kernel(tc, x, w_qkv_words, w_qkv_scales, out):
         ctx.enter_context(tc.manual_schedule())
         keep = ctx.enter_context(tc.tile_pool(name="keep", bufs=1))
         consts = ctx.enter_context(tc.tile_pool(name="consts", bufs=1))
-        x_stage = ctx.enter_context(tc.tile_pool(name="x_stage", bufs=4))
-        g_stage = ctx.enter_context(tc.tile_pool(name="g_stage", bufs=2))
-        w_stage = ctx.enter_context(tc.tile_pool(name="w_stage", bufs=6))
+        x_stage = ctx.enter_context(tc.tile_pool(name="x_stage", bufs=8))
+        g_stage = ctx.enter_context(tc.tile_pool(name="g_stage", bufs=4))
+        w_stage = ctx.enter_context(tc.tile_pool(name="w_stage", bufs=12))
         psum = ctx.enter_context(tc.psum_pool(name="psum", bufs=1))
 
         x_view = x[0].rearrange("(g p t) h w -> p g (t h w)", p=P, t=PACK)
@@ -166,16 +169,17 @@ def tile_relation_k_kernel(tc, x, w_qkv_words, w_qkv_scales, out):
 
         qk_names = ["q0", "q1", "k0", "k1"]
         qk_acc = [psum.tile([P, BANK], F32, name="acc_" + n, tag="bank_" + n) for n in qk_names]
-        raws = [load_x(0), load_x(1)]
-        w_qks = [load_w_qk(0)]
-        raws.append(load_x(2))
-        w_qks.append(load_w_qk(1))
+        raws = [load_x(0)]
+        w_qks = []
+        for c in range(W_LEAD):
+            raws.append(load_x(c + 1))
+            w_qks.append(load_w_qk(c))
         grouped_next = regroup_x(raws[0])
         for c in range(NCHUNK):
-            if c + 3 < NCHUNK:
-                raws.append(load_x(c + 3))
-            if c + 2 < NCHUNK:
-                w_qks.append(load_w_qk(c + 2))
+            if c + X_LEAD < NCHUNK:
+                raws.append(load_x(c + X_LEAD))
+            if c + W_LEAD < NCHUNK:
+                w_qks.append(load_w_qk(c + W_LEAD))
             w_qk = w_qks[c]
             grouped = grouped_next
             if c + 1 < NCHUNK:
@@ -213,13 +217,13 @@ def tile_relation_k_kernel(tc, x, w_qkv_words, w_qkv_scales, out):
                         stop=False,
                     )
 
-        for c in range(NCHUNK):
-            passes = slice(c * CHUNK, (c + 1) * CHUNK)
+        for c in range(PASSES // V_CHUNK):
+            passes = slice(c * V_CHUNK, (c + 1) * V_CHUNK)
             nc.sync.dma_start(out=w_v[:, passes, :].bitcast(I32), in_=words[:, passes, 2 * D : 3 * D])
 
         def v_passes(c):
             for j in range(HALVES):
-                for g in range(c * CHUNK, (c + 1) * CHUNK):
+                for g in range(c * V_CHUNK, (c + 1) * V_CHUNK):
                     mx_pass(
                         v_acc[j][:, 0:PIX],
                         g,
@@ -262,7 +266,7 @@ def tile_relation_k_kernel(tc, x, w_qkv_words, w_qkv_scales, out):
 
         v_tags = ["bank_q0", "bank_k0"]
         v_acc = [psum.tile([P, BANK], F32, name="acc_v%d" % j, tag=v_tags[j]) for j in range(HALVES)]
-        for c in range(NCHUNK):
+        for c in range(PASSES // V_CHUNK):
             v_passes(c)
 
         for b in range(n_tiles // S_PER_BANK):

@@ -28,11 +28,9 @@ NGRP = PIX // GRP
 WIN = 3 * GRP
 CHUNK = 2
 NCHUNK = PASSES // CHUNK
-SLOT = 8
-NSLOT = PASSES // SLOT
-V_CHUNK = 4
-X_LEAD = 6
-W_LEAD = 5
+PLANE_PASSES = 4
+X_LEAD = 5
+W_LEAD = 4
 BANK = 512
 S_PER_BANK = 4
 FAR = -1.0e30
@@ -96,34 +94,30 @@ def tile_relation_k_kernel(tc, x, w_qkv_words, w_qkv_scales, out):
         consts = ctx.enter_context(tc.tile_pool(name="consts", bufs=1))
         x_stage = ctx.enter_context(tc.tile_pool(name="x_stage", bufs=8))
         g_stage = ctx.enter_context(tc.tile_pool(name="g_stage", bufs=4))
-        w_stage = ctx.enter_context(tc.tile_pool(name="w_stage", bufs=12))
+        w_stage = ctx.enter_context(tc.tile_pool(name="w_stage", bufs=10))
         psum = ctx.enter_context(tc.psum_pool(name="psum", bufs=1))
 
         x_view = x[0].rearrange("(g p t) h w -> p g (t h w)", p=P, t=PACK)
         words = w_qkv_words.rearrange("g p n t -> g p (n t)").bitcast(I32).rearrange("g p n -> p g n")
-        scale_rows = w_qkv_scales.bitcast(F32).rearrange("(s g) (quad r) n -> s r quad g n", g=SLOT, r=4)
+        scale_rows = w_qkv_scales.rearrange("(c k) (quad r) n -> quad r k c n", k=PLANE_PASSES, r=4)
         out_view = out[0].rearrange("(j c) h w -> c j (h w)", c=P)
 
-        w_planes = keep.tile([P, PASSES, 3 * D], U8, name="w_planes", align_bytes=64)
+        w_planes = keep.tile([P, PASSES // PLANE_PASSES, 3 * D], U8, name="w_planes", align_bytes=64)
+        nc.vector.memset(w_planes[:].bitcast(I32), 0)
 
-        def clear_planes(s):
-            nc.vector.memset(w_planes[:, s * SLOT : (s + 1) * SLOT, :].bitcast(I32), 0)
-
-        def load_scales(s):
+        def load_scales(quad, queue, dtype):
             for r in range(4):
-                nc.gpsimd.dma_start(
-                    out=w_planes[:].bitcast(F32)[4 * s + r : P : GRP, s * SLOT : (s + 1) * SLOT, :],
-                    in_=scale_rows[s, r],
+                first = 32 * quad + r
+                queue.dma_start(
+                    out=w_planes[:].bitcast(dtype)[first : first + 4 * PLANE_PASSES : 4, :, :],
+                    in_=scale_rows[quad, r].bitcast(dtype),
                 )
 
-        clear_planes(0)
-        load_scales(0)
-        clear_planes(1)
-        load_scales(1)
+        load_scales(2, nc.gpsimd, F32)
+        load_scales(3, nc.gpsimd, F32)
 
         x_codes = keep.tile([P, PASSES, PIX], U32, name="x_codes", align_bytes=64)
         x_planes = keep.tile([P, PASSES, PIX], U8, name="x_planes", align_bytes=64)
-        w_v = keep.tile([P, PASSES, D], U32, name="w_v", align_bytes=64)
         q_diag = keep.tile([P, HALVES, NGRP, P], F32, name="q_diag")
         v_diag = keep.tile([P, HALVES, NGRP, P], F32, name="v_diag")
         k_pad = keep.tile([P, HALVES, (NGRP + 2) * GRP], F32, name="k_pad")
@@ -133,10 +127,10 @@ def tile_relation_k_kernel(tc, x, w_qkv_words, w_qkv_scales, out):
             nc.sync.dma_start(out=raw[:], in_=x_view[:, c * CHUNK : (c + 1) * CHUNK, :])
             return raw
 
-        def load_w_qk(c):
-            w_qk = w_stage.tile([P, CHUNK, 2 * D], U32, name="w_qk", align_bytes=64)
-            nc.sync.dma_start(out=w_qk[:].bitcast(I32), in_=words[:, c * CHUNK : (c + 1) * CHUNK, 0 : 2 * D])
-            return w_qk
+        def load_w(c):
+            w = w_stage.tile([P, CHUNK, 3 * D], U32, name="w", align_bytes=64)
+            nc.sync.dma_start(out=w[:].bitcast(I32), in_=words[:, c * CHUNK : (c + 1) * CHUNK, :])
+            return w
 
         def regroup_x(raw):
             grouped = g_stage.tile([P, CHUNK, PIX * PACK], BF16, name="grouped", align_bytes=64)
@@ -156,81 +150,73 @@ def tile_relation_k_kernel(tc, x, w_qkv_words, w_qkv_scales, out):
                 in_=grouped[:].rearrange("p g e -> p (g e)"),
             )
 
-        def mx_pass(acc, g, w_tile, w_cols, plane_cols):
+        banks = ["q0", "q1", "k0", "k1", "v0", "v1"]
+        acc = [psum.tile([P, BANK], F32, name="acc_" + n, tag="bank_" + n) for n in banks]
+        qk_acc = acc[0 : 2 * HALVES]
+        v_acc = acc[2 * HALVES :]
+
+        def mx_pass(m, g, w, i):
+            c, k = divmod(g, PLANE_PASSES)
+            cols = slice(m * P, (m + 1) * P)
             nc.tensor.matmul_mx(
-                out=acc,
-                lhsT=w_tile[:, w_cols].bitcast(FP8X4),
-                lhsT_scale=w_planes[4 * (g // SLOT) : P, g, plane_cols],
+                out=acc[m][:, 0:PIX],
+                lhsT=w[:, i, cols].bitcast(FP8X4),
+                lhsT_scale=w_planes[4 * k : P, c, cols],
                 rhs=x_codes[:, g, :].bitcast(FP8X4),
                 rhs_scale=x_planes[:, g, :],
                 start=(g == 0),
                 stop=(g == PASSES - 1),
             )
 
-        qk_names = ["q0", "q1", "k0", "k1"]
-        qk_acc = [psum.tile([P, BANK], F32, name="acc_" + n, tag="bank_" + n) for n in qk_names]
+        s_tags = ["bank_s0", "bank_s1", "bank_q0", "bank_k0"]
+
+        def score_bank(b):
+            s_ps = psum.tile([P, S_PER_BANK, WIN], F32, name="s_ps%d" % b, tag=s_tags[b])
+            nc.tensor.matmul(
+                out=s_ps[:].rearrange("p a k -> p (a k)"),
+                lhsT=ident[:],
+                rhs=bias[:].rearrange("p a k -> p (a k)"),
+                start=True,
+                stop=False,
+            )
+            return s_ps
+
         raws = [load_x(0)]
-        w_qks = []
+        ws = []
         for c in range(W_LEAD):
             raws.append(load_x(c + 1))
-            w_qks.append(load_w_qk(c))
+            ws.append(load_w(c))
+            if c % 2 == 1:
+                load_scales(c // 2, nc.sync, I32)
         grouped_next = regroup_x(raws[0])
         for c in range(NCHUNK):
             if c + X_LEAD < NCHUNK:
                 raws.append(load_x(c + X_LEAD))
             if c + W_LEAD < NCHUNK:
-                w_qks.append(load_w_qk(c + W_LEAD))
-            w_qk = w_qks[c]
+                ws.append(load_w(c + W_LEAD))
             grouped = grouped_next
             if c + 1 < NCHUNK:
                 grouped_next = regroup_x(raws[c + 1])
             quantise_x(c, grouped)
-            if c + 2 < NSLOT:
-                clear_planes(c + 2)
-                load_scales(c + 2)
-            if c == NCHUNK // 2:
+            if c == 6:
                 nc.vector.memset(q_diag[:], 0.0)
-                nc.vector.memset(k_pad[:], 0.0)
+            elif c == 7:
                 nc.vector.memset(v_diag[:], 0.0)
+            elif c == 8:
+                nc.vector.memset(k_pad[:], 0.0)
                 bias, n_out, edge = build_constants(nc, consts)
                 ident = consts.tile([P, P], BF16, name="ident")
                 make_identity(nc, ident[:])
                 warm = consts.tile([P, 1], F32, name="warm")
                 nc.scalar.activation(out=warm[:], in_=n_out[:], func=ACT.Exp)
             if c == NCHUNK - 1:
-                order = [(i, m) for m in range(4) for i in range(CHUNK)]
+                order = [(i, m) for m in (0, 2, 1, 3, 4, 5) for i in range(CHUNK)]
             else:
-                order = [(i, m) for i in range(CHUNK) for m in range(4)]
+                order = [(i, m) for i in range(CHUNK) for m in range(len(banks))]
             for i, m in order:
-                cols = slice(m * P, (m + 1) * P)
-                mx_pass(qk_acc[m][:, 0:PIX], c * CHUNK + i, w_qk[:, i, :], cols, cols)
-            if c == NCHUNK // 2 + 1:
-                s_banks = []
-                for b in range(HALVES * NGRP // S_PER_BANK):
-                    s_ps = psum.tile([P, S_PER_BANK, WIN], F32, name="s_ps%d" % b, tag="bank_s%d" % b)
-                    s_banks.append(s_ps)
-                    nc.tensor.matmul(
-                        out=s_ps[:].rearrange("p a k -> p (a k)"),
-                        lhsT=ident[:],
-                        rhs=bias[:].rearrange("p a k -> p (a k)"),
-                        start=True,
-                        stop=False,
-                    )
-
-        for c in range(PASSES // V_CHUNK):
-            passes = slice(c * V_CHUNK, (c + 1) * V_CHUNK)
-            nc.sync.dma_start(out=w_v[:, passes, :].bitcast(I32), in_=words[:, passes, 2 * D : 3 * D])
-
-        def v_passes(c):
-            for j in range(HALVES):
-                for g in range(c * V_CHUNK, (c + 1) * V_CHUNK):
-                    mx_pass(
-                        v_acc[j][:, 0:PIX],
-                        g,
-                        w_v[:, g, :],
-                        slice(j * P, (j + 1) * P),
-                        slice(2 * D + j * P, 2 * D + (j + 1) * P),
-                    )
+                mx_pass(m, c * CHUNK + i, ws[c], i)
+            if c == 9:
+                s_banks = [score_bank(0), score_bank(1)]
 
         n_tiles = HALVES * NGRP
         expd = keep.tile([P, n_tiles, WIN], F32, name="expd", align_bytes=64)
@@ -244,37 +230,36 @@ def tile_relation_k_kernel(tc, x, w_qkv_words, w_qkv_scales, out):
         inv_wide = keep.tile([P, n_tiles, HD], F32, name="inv_wide", align_bytes=64)
         inv_t = keep.tile([P, n_tiles, GRP], F32, name="inv_t", align_bytes=64)
 
-        for j, copy in enumerate([nc.vector.tensor_copy, nc.scalar.copy]):
+        def spread_q(j, copy):
             for head in range(HEADS_T):
                 rows = slice(HD * head, HD * (head + 1))
                 copy(
                     out=q_diag[rows, j, :, HD * head : HD * (head + 1)],
                     in_=qk_acc[j][rows, 0:PIX].rearrange("p (i q) -> p i q", q=GRP),
                 )
+
+        def copy_k(j, copy):
             copy(out=k_pad[:, j, GRP : GRP + PIX], in_=qk_acc[HALVES + j][:, 0:PIX])
 
-        for t in range(n_tiles):
-            j, i = divmod(t, NGRP)
-            b, a = divmod(t, S_PER_BANK)
-            nc.tensor.matmul(
-                out=s_banks[b][:, a, :],
-                lhsT=q_diag[:, j, i, :],
-                rhs=k_pad[:, j, GRP * i : GRP * i + WIN],
-                start=False,
-                stop=(a == S_PER_BANK - 1),
-            )
+        def scores(j):
+            for i in range(NGRP):
+                b, a = divmod(j * NGRP + i, S_PER_BANK)
+                nc.tensor.matmul(
+                    out=s_banks[b][:, a, :],
+                    lhsT=q_diag[:, j, i, :],
+                    rhs=k_pad[:, j, GRP * i : GRP * i + WIN],
+                    start=False,
+                    stop=(a == S_PER_BANK - 1),
+                )
 
-        v_tags = ["bank_q0", "bank_k0"]
-        v_acc = [psum.tile([P, BANK], F32, name="acc_v%d" % j, tag=v_tags[j]) for j in range(HALVES)]
-        for c in range(PASSES // V_CHUNK):
-            v_passes(c)
-
-        for b in range(n_tiles // S_PER_BANK):
+        def top_of(b):
             tiles = slice(b * S_PER_BANK, (b + 1) * S_PER_BANK)
             nc.vector.tensor_reduce(out=top[:, tiles], in_=s_banks[b][:], axis=AXIS_X, op=ALU.max)
             nc.vector.tensor_scalar(
                 out=neg_top[:, tiles], in0=top[:, tiles], scalar1=edge[:, 0:1], scalar2=-1.0, op0=ALU.max, op1=ALU.mult
             )
+
+        def exps(b):
             for a in range(S_PER_BANK):
                 t = b * S_PER_BANK + a
                 nc.scalar.activation(
@@ -285,26 +270,21 @@ def tile_relation_k_kernel(tc, x, w_qkv_words, w_qkv_scales, out):
                     scale=1.0,
                     accum_out=in_sum[:, t : t + 1],
                 )
-        nc.scalar.activation(out=out_exp[:], in_=neg_top[:], func=ACT.Exp, bias=edge[:, 0:1], scale=1.0)
 
-        for j in range(HALVES):
+        def turn_exps(j):
             tiles = slice(j * NGRP, (j + 1) * NGRP)
             nc.vector.transpose(
                 out=expd_t[:, tiles, :].rearrange("p t k -> p (t k)"), in_=expd[:, tiles, :].rearrange("p t k -> p (t k)")
             )
-        nc.vector.scalar_tensor_tensor(
-            out=total[:], in0=out_exp[:], scalar=n_out[:, 0:1], in1=in_sum[:], op0=ALU.mult, op1=ALU.add
-        )
-        nc.vector.reciprocal(out=inv[:], in_=total[:])
-        nc.vector.tensor_copy(out=inv_wide[:], in_=inv[:].unsqueeze(2).to_broadcast([P, n_tiles, HD]))
-        nc.vector.transpose(out=inv_t[:].rearrange("p t q -> p (t q)"), in_=inv_wide[:].rearrange("p t c -> p (t c)"))
 
         v_kc = keep.tile([P, HALVES, PIX], F32, name="v_kc", align_bytes=64)
-        result = keep.tile([P, HALVES, PIX], F32, name="result")
-        for j in range(HALVES):
+
+        def turn_v(j):
             for half in range(2):
                 cols = slice(half * P, (half + 1) * P)
                 nc.vector.transpose(out=v_kc[:, j, cols], in_=v_acc[j][:, cols])
+
+        def spread_v(j):
             for head in range(HEADS_T):
                 rows = slice(HD * head, HD * (head + 1))
                 copy = nc.vector.tensor_copy if head % 2 == 0 else nc.scalar.copy
@@ -312,6 +292,37 @@ def tile_relation_k_kernel(tc, x, w_qkv_words, w_qkv_scales, out):
                     out=v_diag[rows, j, :, HD * head : HD * (head + 1)],
                     in_=v_kc[rows, j, :].rearrange("p (u c) -> p u c", c=HD),
                 )
+
+        spread_q(0, nc.vector.tensor_copy)
+        copy_k(0, nc.scalar.copy)
+        spread_q(1, nc.scalar.copy)
+        copy_k(1, nc.vector.tensor_copy)
+        scores(0)
+        turn_v(0)
+        turn_v(1)
+        s_banks += [score_bank(2), score_bank(3)]
+        scores(1)
+        top_of(0)
+        exps(0)
+        spread_v(0)
+        top_of(1)
+        exps(1)
+        spread_v(1)
+        top_of(2)
+        exps(2)
+        turn_exps(0)
+        top_of(3)
+        exps(3)
+        nc.scalar.activation(out=out_exp[:], in_=neg_top[:], func=ACT.Exp, bias=edge[:, 0:1], scale=1.0)
+        turn_exps(1)
+        nc.vector.scalar_tensor_tensor(
+            out=total[:], in0=out_exp[:], scalar=n_out[:, 0:1], in1=in_sum[:], op0=ALU.mult, op1=ALU.add
+        )
+        nc.vector.reciprocal(out=inv[:], in_=total[:])
+        nc.vector.tensor_copy(out=inv_wide[:], in_=inv[:].unsqueeze(2).to_broadcast([P, n_tiles, HD]))
+        nc.vector.transpose(out=inv_t[:].rearrange("p t q -> p (t q)"), in_=inv_wide[:].rearrange("p t c -> p (t c)"))
+
+        result = keep.tile([P, HALVES, PIX], F32, name="result")
         o_tags = ["bank_q1", "bank_k1"]
         order = [u for first in range(3) for u in range(first, NGRP, 3)]
         for j in range(HALVES):

@@ -29,6 +29,7 @@ WIN = 3 * GRP
 CHUNK = 2
 NCHUNK = PASSES // CHUNK
 PLANE_PASSES = 4
+V_CHUNK = 4
 X_LEAD = 5
 W_LEAD = 4
 BANK = 512
@@ -94,7 +95,7 @@ def tile_relation_k_kernel(tc, x, w_qkv_words, w_qkv_scales, out):
         consts = ctx.enter_context(tc.tile_pool(name="consts", bufs=1))
         x_stage = ctx.enter_context(tc.tile_pool(name="x_stage", bufs=8))
         g_stage = ctx.enter_context(tc.tile_pool(name="g_stage", bufs=4))
-        w_stage = ctx.enter_context(tc.tile_pool(name="w_stage", bufs=10))
+        w_stage = ctx.enter_context(tc.tile_pool(name="w_stage", bufs=14))
         psum = ctx.enter_context(tc.psum_pool(name="psum", bufs=1))
 
         x_view = x[0].rearrange("(g p t) h w -> p g (t h w)", p=P, t=PACK)
@@ -102,6 +103,7 @@ def tile_relation_k_kernel(tc, x, w_qkv_words, w_qkv_scales, out):
         scale_rows = w_qkv_scales.rearrange("(c k) (quad r) n -> quad r k c n", k=PLANE_PASSES, r=4)
         out_view = out[0].rearrange("(j c) h w -> c j (h w)", c=P)
 
+        w_v = keep.tile([P, PASSES, D], U32, name="w_v", align_bytes=64)
         w_planes = keep.tile([P, PASSES // PLANE_PASSES, 3 * D], U8, name="w_planes", align_bytes=64)
         nc.vector.memset(w_planes[:].bitcast(I32), 0)
 
@@ -113,8 +115,8 @@ def tile_relation_k_kernel(tc, x, w_qkv_words, w_qkv_scales, out):
                     in_=scale_rows[quad, r].bitcast(dtype),
                 )
 
-        load_scales(2, nc.gpsimd, F32)
-        load_scales(3, nc.gpsimd, F32)
+        for quad in range(1, 4):
+            load_scales(quad, nc.gpsimd, F32)
 
         x_codes = keep.tile([P, PASSES, PIX], U32, name="x_codes", align_bytes=64)
         x_planes = keep.tile([P, PASSES, PIX], U8, name="x_planes", align_bytes=64)
@@ -128,8 +130,8 @@ def tile_relation_k_kernel(tc, x, w_qkv_words, w_qkv_scales, out):
             return raw
 
         def load_w(c):
-            w = w_stage.tile([P, CHUNK, 3 * D], U32, name="w", align_bytes=64)
-            nc.sync.dma_start(out=w[:].bitcast(I32), in_=words[:, c * CHUNK : (c + 1) * CHUNK, :])
+            w = w_stage.tile([P, CHUNK, 2 * D], U32, name="w", align_bytes=64)
+            nc.sync.dma_start(out=w[:].bitcast(I32), in_=words[:, c * CHUNK : (c + 1) * CHUNK, 0 : 2 * D])
             return w
 
         def regroup_x(raw):
@@ -150,28 +152,23 @@ def tile_relation_k_kernel(tc, x, w_qkv_words, w_qkv_scales, out):
                 in_=grouped[:].rearrange("p g e -> p (g e)"),
             )
 
-        banks = ["q0", "q1", "k0", "k1", "v0", "v1"]
-        acc = [psum.tile([P, BANK], F32, name="acc_" + n, tag="bank_" + n) for n in banks]
-        qk_acc = acc[0 : 2 * HALVES]
-        v_acc = acc[2 * HALVES :]
+        banks = ["q0", "q1", "k0", "k1"]
+        qk_acc = [psum.tile([P, BANK], F32, name="acc_" + n, tag="bank_" + n) for n in banks]
 
-        def mx_pass(m, g, w, i):
+        def mx_pass(acc, m, g, w_tile, first_col):
             c, k = divmod(g, PLANE_PASSES)
-            cols = slice(m * P, (m + 1) * P)
             nc.tensor.matmul_mx(
-                out=acc[m][:, 0:PIX],
-                lhsT=w[:, i, cols].bitcast(FP8X4),
-                lhsT_scale=w_planes[4 * k : P, c, cols],
+                out=acc[:, 0:PIX],
+                lhsT=w_tile[:, m * P - first_col : (m + 1) * P - first_col].bitcast(FP8X4),
+                lhsT_scale=w_planes[4 * k : P, c, m * P : (m + 1) * P],
                 rhs=x_codes[:, g, :].bitcast(FP8X4),
                 rhs_scale=x_planes[:, g, :],
                 start=(g == 0),
                 stop=(g == PASSES - 1),
             )
 
-        s_tags = ["bank_s0", "bank_s1", "bank_q0", "bank_k0"]
-
         def score_bank(b):
-            s_ps = psum.tile([P, S_PER_BANK, WIN], F32, name="s_ps%d" % b, tag=s_tags[b])
+            s_ps = psum.tile([P, S_PER_BANK, WIN], F32, name="s_ps%d" % b, tag="bank_s%d" % b)
             nc.tensor.matmul(
                 out=s_ps[:].rearrange("p a k -> p (a k)"),
                 lhsT=ident[:],
@@ -186,8 +183,8 @@ def tile_relation_k_kernel(tc, x, w_qkv_words, w_qkv_scales, out):
         for c in range(W_LEAD):
             raws.append(load_x(c + 1))
             ws.append(load_w(c))
-            if c % 2 == 1:
-                load_scales(c // 2, nc.sync, I32)
+            if c == 1:
+                load_scales(0, nc.sync, I32)
         grouped_next = regroup_x(raws[0])
         for c in range(NCHUNK):
             if c + X_LEAD < NCHUNK:
@@ -210,13 +207,20 @@ def tile_relation_k_kernel(tc, x, w_qkv_words, w_qkv_scales, out):
                 warm = consts.tile([P, 1], F32, name="warm")
                 nc.scalar.activation(out=warm[:], in_=n_out[:], func=ACT.Exp)
             if c == NCHUNK - 1:
-                order = [(i, m) for m in (0, 2, 1, 3, 4, 5) for i in range(CHUNK)]
+                order = [(i, m) for m in (0, 2, 1, 3) for i in range(CHUNK)]
             else:
                 order = [(i, m) for i in range(CHUNK) for m in range(len(banks))]
             for i, m in order:
-                mx_pass(m, c * CHUNK + i, ws[c], i)
+                mx_pass(qk_acc[m], m, c * CHUNK + i, ws[c][:, i, :], 0)
             if c == 9:
-                s_banks = [score_bank(0), score_bank(1)]
+                s_banks = [score_bank(b) for b in range(HALVES * NGRP // S_PER_BANK)]
+
+        for g in range(0, PASSES, V_CHUNK):
+            nc.sync.dma_start(out=w_v[:, g : g + V_CHUNK, :].bitcast(I32), in_=words[:, g : g + V_CHUNK, 2 * D : 3 * D])
+
+        def v_passes(j, passes):
+            for g in passes:
+                mx_pass(v_acc[j], 2 * HALVES + j, g, w_v[:, g, :], 2 * D)
 
         n_tiles = HALVES * NGRP
         expd = keep.tile([P, n_tiles, WIN], F32, name="expd", align_bytes=64)
@@ -298,21 +302,17 @@ def tile_relation_k_kernel(tc, x, w_qkv_words, w_qkv_scales, out):
         spread_q(1, nc.scalar.copy)
         copy_k(1, nc.vector.tensor_copy)
         scores(0)
-        turn_v(0)
-        turn_v(1)
-        s_banks += [score_bank(2), score_bank(3)]
         scores(1)
-        top_of(0)
-        exps(0)
-        spread_v(0)
-        top_of(1)
-        exps(1)
-        spread_v(1)
-        top_of(2)
-        exps(2)
+        for b in range(n_tiles // S_PER_BANK):
+            top_of(b)
+            exps(b)
+        v_acc = [psum.tile([P, BANK], F32, name="acc_v%d" % j, tag="bank_k%d" % j) for j in range(HALVES)]
+        for g in range(0, 3 * PASSES // 4, V_CHUNK):
+            for j in range(HALVES):
+                v_passes(j, range(g, g + V_CHUNK))
+        for j in range(HALVES):
+            v_passes(j, range(3 * PASSES // 4, PASSES))
         turn_exps(0)
-        top_of(3)
-        exps(3)
         nc.scalar.activation(out=out_exp[:], in_=neg_top[:], func=ACT.Exp, bias=edge[:, 0:1], scale=1.0)
         turn_exps(1)
         nc.vector.scalar_tensor_tensor(
@@ -322,8 +322,11 @@ def tile_relation_k_kernel(tc, x, w_qkv_words, w_qkv_scales, out):
         nc.vector.tensor_copy(out=inv_wide[:], in_=inv[:].unsqueeze(2).to_broadcast([P, n_tiles, HD]))
         nc.vector.transpose(out=inv_t[:].rearrange("p t q -> p (t q)"), in_=inv_wide[:].rearrange("p t c -> p (t c)"))
 
+        for j in range(HALVES):
+            turn_v(j)
+            spread_v(j)
         result = keep.tile([P, HALVES, PIX], F32, name="result")
-        o_tags = ["bank_q1", "bank_k1"]
+        o_tags = ["bank_q0", "bank_q1"]
         order = [u for first in range(3) for u in range(first, NGRP, 3)]
         for j in range(HALVES):
             o_ps = psum.tile([P, BANK], F32, name="o_ps%d" % j, tag=o_tags[j])

@@ -28,10 +28,12 @@ NGRP = PIX // GRP
 WIN = 3 * GRP
 CHUNK = 2
 NCHUNK = PASSES // CHUNK
+LOAD = 4
+NLOAD = PASSES // LOAD
 PLANE_PASSES = 4
 V_CHUNK = 4
-X_LEAD = 5
-W_LEAD = 4
+X_LEAD = 4
+W_LEAD = 3
 BANK = 512
 S_PER_BANK = 4
 FAR = -1.0e30
@@ -93,9 +95,9 @@ def tile_relation_k_kernel(tc, x, w_qkv_words, w_qkv_scales, out):
         ctx.enter_context(tc.manual_schedule())
         keep = ctx.enter_context(tc.tile_pool(name="keep", bufs=1))
         consts = ctx.enter_context(tc.tile_pool(name="consts", bufs=1))
-        x_stage = ctx.enter_context(tc.tile_pool(name="x_stage", bufs=8))
+        x_stage = ctx.enter_context(tc.tile_pool(name="x_stage", bufs=4))
         g_stage = ctx.enter_context(tc.tile_pool(name="g_stage", bufs=4))
-        w_stage = ctx.enter_context(tc.tile_pool(name="w_stage", bufs=14))
+        w_stage = ctx.enter_context(tc.tile_pool(name="w_stage", bufs=7))
         psum = ctx.enter_context(tc.psum_pool(name="psum", bufs=1))
 
         x_view = x[0].rearrange("(g p t) h w -> p g (t h w)", p=P, t=PACK)
@@ -115,7 +117,7 @@ def tile_relation_k_kernel(tc, x, w_qkv_words, w_qkv_scales, out):
                     in_=scale_rows[quad, r].bitcast(dtype),
                 )
 
-        for quad in range(1, 4):
+        for quad in range(2, 4):
             load_scales(quad, nc.gpsimd, F32)
 
         x_codes = keep.tile([P, PASSES, PIX], U32, name="x_codes", align_bytes=64)
@@ -124,23 +126,27 @@ def tile_relation_k_kernel(tc, x, w_qkv_words, w_qkv_scales, out):
         v_diag = keep.tile([P, HALVES, NGRP, P], F32, name="v_diag")
         k_pad = keep.tile([P, HALVES, (NGRP + 2) * GRP], F32, name="k_pad")
 
-        def load_x(c):
-            raw = x_stage.tile([P, CHUNK, PACK * PIX], BF16, name="raw")
-            nc.sync.dma_start(out=raw[:], in_=x_view[:, c * CHUNK : (c + 1) * CHUNK, :])
+        def load_x(n):
+            raw = x_stage.tile([P, LOAD, PACK * PIX], BF16, name="raw")
+            nc.sync.dma_start(out=raw[:], in_=x_view[:, n * LOAD : (n + 1) * LOAD, :])
             return raw
 
-        def load_w(c):
-            w = w_stage.tile([P, CHUNK, 2 * D], U32, name="w", align_bytes=64)
-            nc.sync.dma_start(out=w[:].bitcast(I32), in_=words[:, c * CHUNK : (c + 1) * CHUNK, 0 : 2 * D])
+        def load_w(n):
+            w = w_stage.tile([P, LOAD, 2 * D], U32, name="w", align_bytes=64)
+            part = LOAD if n < NLOAD - 2 else LOAD // 2
+            for i in range(0, LOAD, part):
+                g = n * LOAD + i
+                nc.sync.dma_start(out=w[:, i : i + part, :].bitcast(I32), in_=words[:, g : g + part, 0 : 2 * D])
             return w
 
-        def regroup_x(raw):
+        def regroup_x(c):
             grouped = g_stage.tile([P, CHUNK, PIX * PACK], BF16, name="grouped", align_bytes=64)
+            n, first = divmod(c * CHUNK, LOAD)
             for i in range(CHUNK):
                 copy = nc.vector.tensor_copy if i % 2 == 0 else nc.scalar.copy
                 copy(
                     out=grouped[:, i, :].rearrange("p (c i t) -> p c t i", i=4, t=PACK),
-                    in_=raw[:, i, :].rearrange("p (t c i) -> p c t i", t=PACK, i=4),
+                    in_=raws[n][:, first + i, :].rearrange("p (t c i) -> p c t i", t=PACK, i=4),
                 )
             return grouped
 
@@ -180,20 +186,22 @@ def tile_relation_k_kernel(tc, x, w_qkv_words, w_qkv_scales, out):
 
         raws = [load_x(0)]
         ws = []
-        for c in range(W_LEAD):
-            raws.append(load_x(c + 1))
-            ws.append(load_w(c))
-            if c == 1:
-                load_scales(0, nc.sync, I32)
-        grouped_next = regroup_x(raws[0])
+        for n in range(W_LEAD):
+            raws.append(load_x(n + 1))
+            ws.append(load_w(n))
+            if n < 2:
+                load_scales(n, nc.sync, I32)
+        grouped_next = regroup_x(0)
         for c in range(NCHUNK):
-            if c + X_LEAD < NCHUNK:
-                raws.append(load_x(c + X_LEAD))
-            if c + W_LEAD < NCHUNK:
-                ws.append(load_w(c + W_LEAD))
             grouped = grouped_next
             if c + 1 < NCHUNK:
-                grouped_next = regroup_x(raws[c + 1])
+                grouped_next = regroup_x(c + 1)
+            n, first = divmod(c * CHUNK, LOAD)
+            if first == LOAD - CHUNK:
+                if n + X_LEAD < NLOAD:
+                    raws.append(load_x(n + X_LEAD))
+                if n + W_LEAD < NLOAD:
+                    ws.append(load_w(n + W_LEAD))
             quantise_x(c, grouped)
             if c == 6:
                 nc.vector.memset(q_diag[:], 0.0)
@@ -211,7 +219,7 @@ def tile_relation_k_kernel(tc, x, w_qkv_words, w_qkv_scales, out):
             else:
                 order = [(i, m) for i in range(CHUNK) for m in range(len(banks))]
             for i, m in order:
-                mx_pass(qk_acc[m], m, c * CHUNK + i, ws[c][:, i, :], 0)
+                mx_pass(qk_acc[m], m, c * CHUNK + i, ws[n][:, first + i, :], 0)
             if c == 9:
                 s_banks = [score_bank(b) for b in range(HALVES * NGRP // S_PER_BANK)]
 

from contextlib import ExitStack

import concourse.mybir as mybir
from concourse.masks import make_identity

F32 = mybir.dt.float32
BF16 = mybir.dt.bfloat16
I32 = mybir.dt.int32
U32 = mybir.dt.uint32
U8 = mybir.dt.uint8
FP8X4 = mybir.dt.float8_e4m3fn_x4
ALU = mybir.AluOpType
ACT = mybir.ActivationFunctionType
AXIS_X = mybir.AxisListType.X

P = 128
PACK = 4
C_IN = 16384
PASSES = C_IN // (P * PACK)
PIX = 256
WIDTH = 16
D = 256
HALVES = D // P
HEADS_T = 4
HD = 32
GRP = 32
NGRP = PIX // GRP
WIN = 3 * GRP
CHUNK = 2
NCHUNK = PASSES // CHUNK
LOAD = 4
NLOAD = PASSES // LOAD
PLANE_PASSES = 4
V_CHUNK = 4
X_LEAD = 4
W_LEAD = 3
BANK = 512
S_PER_BANK = 4
FAR = -1.0e30

FLOPS = 2 * C_IN * 3 * D * PIX + 2 * 2 * PIX * 25 * D


def build_constants(nc, consts):
    part_i = consts.tile([P, 1], I32, name="part_i")
    nc.gpsimd.iota(part_i[:], pattern=[[0, 1]], base=0, channel_multiplier=1)
    key_col_i = consts.tile([P, WIN], I32, name="key_col_i")
    nc.gpsimd.iota(key_col_i[:], pattern=[[0, WIN // WIDTH], [1, WIDTH]], base=0, channel_multiplier=0)
    key_row_i = consts.tile([P, WIN], I32, name="key_row_i")
    nc.gpsimd.iota(key_row_i[:], pattern=[[1, WIN // WIDTH], [0, WIDTH]], base=0, channel_multiplier=0)

    q_col_i = consts.tile([P, 1], I32, name="q_col_i")
    nc.vector.tensor_scalar(out=q_col_i[:], in0=part_i[:], scalar1=WIDTH - 1, scalar2=None, op0=ALU.bitwise_and)
    q_row_i = consts.tile([P, 1], I32, name="q_row_i")
    nc.vector.tensor_scalar(
        out=q_row_i[:], in0=part_i[:], scalar1=4, scalar2=1, op0=ALU.logical_shift_right, op1=ALU.bitwise_and
    )
    q_col = consts.tile([P, 1], F32, name="q_col")
    nc.vector.tensor_copy(out=q_col[:], in_=q_col_i[:])
    q_row = consts.tile([P, 1], F32, name="q_row")
    nc.vector.tensor_scalar(out=q_row[:], in0=q_row_i[:], scalar1=2.0, scalar2=None, op0=ALU.add)

    d_col = consts.tile([P, WIN], F32, name="d_col")
    nc.vector.tensor_scalar(out=d_col[:], in0=key_col_i[:], scalar1=q_col[:, 0:1], scalar2=None, op0=ALU.subtract)
    d_row = consts.tile([P, WIN], F32, name="d_row")
    nc.vector.tensor_scalar(out=d_row[:], in0=key_row_i[:], scalar1=q_row[:, 0:1], scalar2=None, op0=ALU.subtract)
    nc.vector.tensor_tensor(out=d_col[:], in0=d_col[:], in1=d_col[:], op=ALU.mult)
    nc.vector.tensor_tensor(out=d_row[:], in0=d_row[:], in1=d_row[:], op=ALU.mult)
    nc.vector.tensor_tensor(out=d_col[:], in0=d_col[:], in1=d_row[:], op=ALU.max)
    bias = consts.tile([P, S_PER_BANK, WIN], BF16, name="bias")
    nc.vector.tensor_scalar(
        out=bias[:],
        in0=d_col[:].unsqueeze(1).to_broadcast([P, S_PER_BANK, WIN]),
        scalar1=4.5,
        scalar2=FAR,
        op0=ALU.is_gt,
        op1=ALU.mult,
    )

    left = consts.tile([P, 1], F32, name="left")
    nc.vector.tensor_scalar(out=left[:], in0=q_col[:], scalar1=-1.0, scalar2=2.0, op0=ALU.mult, op1=ALU.add)
    right = consts.tile([P, 1], F32, name="right")
    nc.vector.tensor_scalar(out=right[:], in0=q_col[:], scalar1=float(WIDTH - 3), scalar2=None, op0=ALU.subtract)
    nc.vector.tensor_tensor(out=left[:], in0=left[:], in1=right[:], op=ALU.max)
    n_out = consts.tile([P, 1], F32, name="n_out")
    nc.vector.tensor_scalar(out=n_out[:], in0=left[:], scalar1=0.0, scalar2=5.0, op0=ALU.max, op1=ALU.mult)
    edge = consts.tile([P, 1], F32, name="edge")
    nc.vector.tensor_scalar(out=edge[:], in0=n_out[:], scalar1=0.5, scalar2=FAR, op0=ALU.is_lt, op1=ALU.mult)
    return bias, n_out, edge


def tile_relation_k_kernel(tc, x, w_qkv_words, w_qkv_scales, out):
    nc = tc.nc
    with ExitStack() as ctx:
        ctx.enter_context(tc.manual_schedule())
        keep = ctx.enter_context(tc.tile_pool(name="keep", bufs=1))
        consts = ctx.enter_context(tc.tile_pool(name="consts", bufs=1))
        x_stage = ctx.enter_context(tc.tile_pool(name="x_stage", bufs=4))
        g_stage = ctx.enter_context(tc.tile_pool(name="g_stage", bufs=4))
        w_stage = ctx.enter_context(tc.tile_pool(name="w_stage", bufs=7))
        psum = ctx.enter_context(tc.psum_pool(name="psum", bufs=1))

        x_view = x[0].rearrange("(g p t) h w -> p g (t h w)", p=P, t=PACK)
        words = w_qkv_words.rearrange("g p n t -> g p (n t)").bitcast(I32).rearrange("g p n -> p g n")
        scale_rows = w_qkv_scales.rearrange("(c k) (quad r) n -> quad r k c n", k=PLANE_PASSES, r=4)
        out_view = out[0].rearrange("(j c) h w -> c j (h w)", c=P)

        w_v = keep.tile([P, PASSES, D], U32, name="w_v", align_bytes=64)
        w_planes = keep.tile([P, PASSES // PLANE_PASSES, 3 * D], U8, name="w_planes", align_bytes=64)
        nc.vector.memset(w_planes[:].bitcast(I32), 0)

        def load_scales(quad, queue, dtype):
            for r in range(4):
                first = 32 * quad + r
                queue.dma_start(
                    out=w_planes[:].bitcast(dtype)[first : first + 4 * PLANE_PASSES : 4, :, :],
                    in_=scale_rows[quad, r].bitcast(dtype),
                )

        for quad in range(2, 4):
            load_scales(quad, nc.gpsimd, F32)

        x_codes = keep.tile([P, PASSES, PIX], U32, name="x_codes", align_bytes=64)
        x_planes = keep.tile([P, PASSES, PIX], U8, name="x_planes", align_bytes=64)
        q_diag = keep.tile([P, HALVES, NGRP, P], F32, name="q_diag")
        v_diag = keep.tile([P, HALVES, NGRP, P], F32, name="v_diag")
        k_pad = keep.tile([P, HALVES, (NGRP + 2) * GRP], F32, name="k_pad")

        def load_x(n):
            raw = x_stage.tile([P, LOAD, PACK * PIX], BF16, name="raw")
            nc.sync.dma_start(out=raw[:], in_=x_view[:, n * LOAD : (n + 1) * LOAD, :])
            return raw

        def load_w(n):
            w = w_stage.tile([P, LOAD, 2 * D], U32, name="w", align_bytes=64)
            part = LOAD if n < NLOAD - 2 else LOAD // 2
            for i in range(0, LOAD, part):
                g = n * LOAD + i
                nc.sync.dma_start(out=w[:, i : i + part, :].bitcast(I32), in_=words[:, g : g + part, 0 : 2 * D])
            return w

        def regroup_x(c):
            grouped = g_stage.tile([P, CHUNK, PIX * PACK], BF16, name="grouped", align_bytes=64)
            n, first = divmod(c * CHUNK, LOAD)
            for i in range(CHUNK):
                copy = nc.vector.tensor_copy if i % 2 == 0 else nc.scalar.copy
                copy(
                    out=grouped[:, i, :].rearrange("p (c i t) -> p c t i", i=4, t=PACK),
                    in_=raws[n][:, first + i, :].rearrange("p (t c i) -> p c t i", t=PACK, i=4),
                )
            return grouped

        def quantise_x(c, grouped):
            passes = slice(c * CHUNK, (c + 1) * CHUNK)
            nc.vector.quantize_mx(
                out=x_codes[:, passes, :].rearrange("p g w -> p (g w)").bitcast(FP8X4),
                scales=x_planes[:, passes, :].rearrange("p g w -> p (g w)"),
                in_=grouped[:].rearrange("p g e -> p (g e)"),
            )

        banks = ["q0", "q1", "k0", "k1"]
        qk_acc = [psum.tile([P, BANK], F32, name="acc_" + n, tag="bank_" + n) for n in banks]

        def mx_pass(acc, m, g, w_tile, first_col):
            c, k = divmod(g, PLANE_PASSES)
            nc.tensor.matmul_mx(
                out=acc[:, 0:PIX],
                lhsT=w_tile[:, m * P - first_col : (m + 1) * P - first_col].bitcast(FP8X4),
                lhsT_scale=w_planes[4 * k : P, c, m * P : (m + 1) * P],
                rhs=x_codes[:, g, :].bitcast(FP8X4),
                rhs_scale=x_planes[:, g, :],
                start=(g == 0),
                stop=(g == PASSES - 1),
            )

        def score_bank(b):
            s_ps = psum.tile([P, S_PER_BANK, WIN], F32, name="s_ps%d" % b, tag="bank_s%d" % b)
            nc.tensor.matmul(
                out=s_ps[:].rearrange("p a k -> p (a k)"),
                lhsT=ident[:],
                rhs=bias[:].rearrange("p a k -> p (a k)"),
                start=True,
                stop=False,
            )
            return s_ps

        raws = [load_x(0)]
        ws = []
        for n in range(W_LEAD):
            raws.append(load_x(n + 1))
            ws.append(load_w(n))
            if n < 2:
                load_scales(n, nc.sync, I32)
        grouped_next = regroup_x(0)
        for c in range(NCHUNK):
            grouped = grouped_next
            if c + 1 < NCHUNK:
                grouped_next = regroup_x(c + 1)
            n, first = divmod(c * CHUNK, LOAD)
            if first == LOAD - CHUNK:
                if n + X_LEAD < NLOAD:
                    raws.append(load_x(n + X_LEAD))
                if n + W_LEAD < NLOAD:
                    ws.append(load_w(n + W_LEAD))
            quantise_x(c, grouped)
            if c == 6:
                nc.vector.memset(q_diag[:], 0.0)
            elif c == 7:
                nc.vector.memset(v_diag[:], 0.0)
            elif c == 8:
                nc.vector.memset(k_pad[:], 0.0)
                bias, n_out, edge = build_constants(nc, consts)
                ident = consts.tile([P, P], BF16, name="ident")
                make_identity(nc, ident[:])
                warm = consts.tile([P, 1], F32, name="warm")
                nc.scalar.activation(out=warm[:], in_=n_out[:], func=ACT.Exp)
            if c == NCHUNK - 1:
                order = [(i, m) for m in (0, 2, 1, 3) for i in range(CHUNK)]
            else:
                order = [(i, m) for i in range(CHUNK) for m in range(len(banks))]
            for i, m in order:
                mx_pass(qk_acc[m], m, c * CHUNK + i, ws[n][:, first + i, :], 0)
            if c == 9:
                s_banks = [score_bank(b) for b in range(HALVES * NGRP // S_PER_BANK)]

        for g in range(0, PASSES, V_CHUNK):
            nc.sync.dma_start(out=w_v[:, g : g + V_CHUNK, :].bitcast(I32), in_=words[:, g : g + V_CHUNK, 2 * D : 3 * D])

        def v_passes(j, passes):
            for g in passes:
                mx_pass(v_acc[j], 2 * HALVES + j, g, w_v[:, g, :], 2 * D)

        n_tiles = HALVES * NGRP
        expd = keep.tile([P, n_tiles, WIN], F32, name="expd", align_bytes=64)
        expd_t = keep.tile([P, n_tiles, WIN], F32, name="expd_t", align_bytes=64)
        top = keep.tile([P, n_tiles], F32, name="top")
        neg_top = keep.tile([P, n_tiles], F32, name="neg_top")
        in_sum = keep.tile([P, n_tiles], F32, name="in_sum")
        out_exp = keep.tile([P, n_tiles], F32, name="out_exp")
        total = keep.tile([P, n_tiles], F32, name="total")
        inv = keep.tile([P, n_tiles], F32, name="inv")
        inv_wide = keep.tile([P, n_tiles, HD], F32, name="inv_wide", align_bytes=64)
        inv_t = keep.tile([P, n_tiles, GRP], F32, name="inv_t", align_bytes=64)

        def spread_q(j, copy):
            for head in range(HEADS_T):
                rows = slice(HD * head, HD * (head + 1))
                copy(
                    out=q_diag[rows, j, :, HD * head : HD * (head + 1)],
                    in_=qk_acc[j][rows, 0:PIX].rearrange("p (i q) -> p i q", q=GRP),
                )

        def copy_k(j, copy):
            copy(out=k_pad[:, j, GRP : GRP + PIX], in_=qk_acc[HALVES + j][:, 0:PIX])

        def scores(j):
            for i in range(NGRP):
                b, a = divmod(j * NGRP + i, S_PER_BANK)
                nc.tensor.matmul(
                    out=s_banks[b][:, a, :],
                    lhsT=q_diag[:, j, i, :],
                    rhs=k_pad[:, j, GRP * i : GRP * i + WIN],
                    start=False,
                    stop=(a == S_PER_BANK - 1),
                )

        def top_of(b):
            tiles = slice(b * S_PER_BANK, (b + 1) * S_PER_BANK)
            nc.vector.tensor_reduce(out=top[:, tiles], in_=s_banks[b][:], axis=AXIS_X, op=ALU.max)
            nc.vector.tensor_scalar(
                out=neg_top[:, tiles], in0=top[:, tiles], scalar1=edge[:, 0:1], scalar2=-1.0, op0=ALU.max, op1=ALU.mult
            )

        def exps(b):
            for a in range(S_PER_BANK):
                t = b * S_PER_BANK + a
                nc.scalar.activation(
                    out=expd[:, t, :],
                    in_=s_banks[b][:, a, :],
                    func=ACT.Exp,
                    bias=neg_top[:, t : t + 1],
                    scale=1.0,
                    accum_out=in_sum[:, t : t + 1],
                )

        def turn_exps(j):
            tiles = slice(j * NGRP, (j + 1) * NGRP)
            nc.vector.transpose(
                out=expd_t[:, tiles, :].rearrange("p t k -> p (t k)"), in_=expd[:, tiles, :].rearrange("p t k -> p (t k)")
            )

        v_kc = keep.tile([P, HALVES, PIX], F32, name="v_kc", align_bytes=64)

        def turn_v(j):
            for half in range(2):
                cols = slice(half * P, (half + 1) * P)
                nc.vector.transpose(out=v_kc[:, j, cols], in_=v_acc[j][:, cols])

        def spread_v(j):
            for head in range(HEADS_T):
                rows = slice(HD * head, HD * (head + 1))
                copy = nc.vector.tensor_copy if head % 2 == 0 else nc.scalar.copy
                copy(
                    out=v_diag[rows, j, :, HD * head : HD * (head + 1)],
                    in_=v_kc[rows, j, :].rearrange("p (u c) -> p u c", c=HD),
                )

        spread_q(0, nc.vector.tensor_copy)
        copy_k(0, nc.scalar.copy)
        spread_q(1, nc.scalar.copy)
        copy_k(1, nc.vector.tensor_copy)
        scores(0)
        scores(1)
        for b in range(n_tiles // S_PER_BANK):
            top_of(b)
            exps(b)
        v_acc = [psum.tile([P, BANK], F32, name="acc_v%d" % j, tag="bank_k%d" % j) for j in range(HALVES)]
        for g in range(0, 3 * PASSES // 4, V_CHUNK):
            for j in range(HALVES):
                v_passes(j, range(g, g + V_CHUNK))
        for j in range(HALVES):
            v_passes(j, range(3 * PASSES // 4, PASSES))
        turn_exps(0)
        nc.scalar.activation(out=out_exp[:], in_=neg_top[:], func=ACT.Exp, bias=edge[:, 0:1], scale=1.0)
        turn_exps(1)
        nc.vector.scalar_tensor_tensor(
            out=total[:], in0=out_exp[:], scalar=n_out[:, 0:1], in1=in_sum[:], op0=ALU.mult, op1=ALU.add
        )
        nc.vector.reciprocal(out=inv[:], in_=total[:])
        nc.vector.tensor_copy(out=inv_wide[:], in_=inv[:].unsqueeze(2).to_broadcast([P, n_tiles, HD]))
        nc.vector.transpose(out=inv_t[:].rearrange("p t q -> p (t q)"), in_=inv_wide[:].rearrange("p t c -> p (t c)"))

        for j in range(HALVES):
            turn_v(j)
            spread_v(j)
        result = keep.tile([P, HALVES, PIX], F32, name="result")
        o_tags = ["bank_q0", "bank_q1"]
        order = [u for first in range(3) for u in range(first, NGRP, 3)]
        for j in range(HALVES):
            o_ps = psum.tile([P, BANK], F32, name="o_ps%d" % j, tag=o_tags[j])
            exp_j = expd_t[:, j * NGRP : (j + 1) * NGRP, :].rearrange("p t k -> p (t k)")
            for n, u in enumerate(order):
                lo = max(u - 1, 0)
                hi = min(u + 1, NGRP - 1)
                count = hi - lo + 1
                start_col = WIN * lo + GRP * (u - lo + 1)
                nc.tensor.matmul(
                    out=o_ps[:, GRP * lo : GRP * (hi + 1)].rearrange("p (d q) -> p d q", q=GRP),
                    lhsT=v_diag[:, j, u, :],
                    rhs=exp_j[:, start_col : start_col + 2 * GRP * count].rearrange("p (d w) -> p d w", w=2 * GRP)[
                        :, :, 0:GRP
                    ],
                    start=(n == 0),
                    stop=(n == NGRP - 1),
                )
            nc.vector.tensor_tensor(
                out=result[:, j, :],
                in0=o_ps[:, 0:PIX],
                in1=inv_t[:, j * NGRP : (j + 1) * NGRP, :].rearrange("p t q -> p (t q)"),
                op=ALU.mult,
            )
            nc.sync.dma_start(out=out_view[:, j, :], in_=result[:, j, :])
